import numpy as np
import ml_dtypes


def mxq(x, axis, fmt="e4m3"):
    dtype, down = {"e4m3": (ml_dtypes.float8_e4m3fn, 7), "e5m2": (ml_dtypes.float8_e5m2, 14)}[fmt]
    v = np.moveaxis(np.asarray(x, np.float32).astype(ml_dtypes.bfloat16).astype(np.float64), axis, -1)
    blocks = v.reshape(v.shape[:-1] + (-1, 32))
    amax = np.abs(blocks).max(-1, keepdims=True)
    byte = np.maximum(np.where(amax > 0, np.frexp(amax)[1] - 1 + 127, 0) - down, 1)
    scale = np.exp2(byte - 127.0)
    codes = (blocks / scale).astype(np.float32).astype(dtype).astype(np.float64)
    return np.moveaxis((codes * scale).reshape(v.shape), -1, axis)


WIDE = False


def mx_kscale(k):
    if not WIDE:
        return np.ones(k)
    levels = np.array([10, -10, 5, -5, 0])
    if k % 512:
        return np.exp2(np.random.permutation(np.resize(levels, k // 32))).repeat(32)
    a = np.empty((k // 512, 16))
    for p in range(k // 512):
        a[p, :8] = np.random.permutation(np.resize(levels, 8))
        for g in range(8):
            far = levels[np.abs(levels - a[p, g]) >= 10]
            a[p, g + 8] = far[np.random.randint(len(far))]
    return np.exp2(a.ravel()).repeat(32)


BF16 = ml_dtypes.bfloat16


def bf(x):
    return np.asarray(x, np.float32).astype(BF16)


def f64(x):
    return np.asarray(x).astype(np.float64)


B, S, IN_DIM, OUT_DIM, MOD_DIM = 4, 64, 8192, 1024, 512
EPS = 1e-8
GAIN = np.sqrt(2.0 / (1.0 + 0.2 ** 2))


def setup_inputs():
    ks = mx_kscale(MOD_DIM)
    kt = mx_kscale(IN_DIM)
    return {"x": bf(np.random.standard_normal((B, S, IN_DIM))),
            "modulation": bf(np.random.standard_normal((B, S, MOD_DIM)) * ks),
            "weight": bf(np.random.standard_normal((OUT_DIM, IN_DIM)) * GAIN / np.sqrt(IN_DIM) / kt[None, :]),
            "bias": bf(np.random.standard_normal(OUT_DIM) * 0.1),
            "mod_w": bf(np.random.standard_normal((IN_DIM, MOD_DIM)) / np.sqrt(MOD_DIM) * kt[:, None] / ks[None, :]),
            "mod_b": bf((1.0 + 0.1 * np.random.standard_normal(IN_DIM)) * kt)}


def reference(x, modulation, weight, bias, mod_w, mod_b):
    xf, w = f64(x), f64(weight)
    s = (mxq(f64(modulation), 2, "e4m3") @ mxq(f64(mod_w), 1, "e4m3").T) + f64(mod_b)
    out = mxq(xf * s, 2, "e4m3") @ mxq(w, 1, "e4m3").T
    demod = 1.0 / np.sqrt((mxq(s * s, 2, "e4m3") @ mxq(w * w, 1, "e4m3").T) + EPS)
    return out * demod + f64(bias)

@@ -1,0 +1,402 @@
+from contextlib import ExitStack
+
+import concourse.mybir as mybir
+from concourse.masks import make_identity
+
+F32 = mybir.dt.float32
+BF16 = mybir.dt.bfloat16
+U32 = mybir.dt.uint32
+U8 = mybir.dt.uint8
+FP8X4 = mybir.dt.float8_e4m3fn_x4
+ACT = mybir.ActivationFunctionType
+ALU = mybir.AluOpType
+
+P = 128
+TOKENS = 256
+IN_DIM = 8192
+OUT_DIM = 1024
+MOD_DIM = 512
+EPS = 1e-8
+
+K_PASS = 512
+PASSES = IN_DIM // K_PASS
+WORDS = K_PASS // 2
+BANK = 512
+TOKEN_TILES = TOKENS // P
+ROUND_OUT = 512
+ROUNDS = OUT_DIM // ROUND_OUT
+ROW_TILES = ROUND_OUT // P
+W_PASSES = ROUNDS * PASSES
+
+X_LOAD = 2
+W_LOAD = 2
+AHEAD = 3
+PAIR = 2
+PAIR_COLS = PAIR * ROUND_OUT * 4
+W_PAIRS = W_PASSES // PAIR
+ROUND_PAIRS = PASSES // PAIR
+STAGE1_TURNS = PASSES + 4
+W_LAG = 2
+W_EARLY = STAGE1_TURNS - W_LAG
+KEPT_PAIRS = W_EARLY // PAIR
+
+SQUARE_COLS_VECTOR = 2176
+
+FLOPS = 2 * TOKENS * (MOD_DIM * IN_DIM + 2 * IN_DIM * OUT_DIM)
+
+
+def transpose_words(nc, bank_cols, rows_bf16, first_word, u, ident):
+    nc.tensor.transpose(
+        bank_cols, rows_bf16.bitcast(F32)[:, first_word + u : first_word + WORDS : 2], ident
+    )
+
+
+def tile_modulatedlinear_k_kernel(tc, x, modulation, weight, bias, mod_w, mod_b, out):
+    nc = tc.nc
+    x_rows = x.flatten_outer_dims().rearrange("(a r) i -> r a i", r=P)
+    modulation_rows = modulation.flatten_outer_dims().rearrange("(a r) k -> r a k", r=P)
+    out_rows = out.flatten_outer_dims()
+    mod_w_rows = mod_w.rearrange("(g r j) k -> r g j k", r=P, j=4)
+    weight_rows = weight.rearrange("(h b r) i -> r h b i", b=ROW_TILES, r=P)
+
+    with ExitStack() as whole:
+        whole.enter_context(tc.manual_schedule())
+        const = whole.enter_context(tc.tile_pool(name="const", bufs=1))
+        w_in = whole.enter_context(tc.tile_pool(name="w_in", bufs=3))
+        w_kept = whole.enter_context(tc.tile_pool(name="w_kept", bufs=KEPT_PAIRS))
+        w_turned = whole.enter_context(tc.psum_pool(name="w_turned", bufs=2))
+
+        ident = const.tile([P, P], F32)
+        make_identity(nc, ident[:])
+        eps = const.tile([P, 1], F32)
+        nc.vector.memset(eps[:], EPS)
+        table_warm = const.tile([P, 1], F32)
+        nc.scalar.activation(out=table_warm[:], in_=eps[:], func=ACT.Abs_reciprocal_sqrt)
+
+        bias_all = const.tile([P, OUT_DIM], BF16)
+        nc.gpsimd.dma_start(out=bias_all[:], in_=bias.partition_broadcast(P))
+
+        prod_codes = const.tile([P, PASSES * 2 * TOKENS], U32, align_bytes=64)
+        prod_scales = const.tile([P, PASSES * 2 * TOKENS], U8, align_bytes=64)
+        mod_b_cols = const.tile([P, 4 * PASSES], F32)
+
+        w_raw = {}
+        w_grouped = {}
+
+        def load_weight(load):
+            first = load * W_LOAD
+            raw = w_in.tile([P, ROW_TILES, W_LOAD * K_PASS], BF16, name="w_raw")
+            nc.sync.dma_start(
+                out=raw[:],
+                in_=weight_rows[
+                    :, first // PASSES, :,
+                    (first % PASSES) * K_PASS : (first % PASSES + W_LOAD) * K_PASS,
+                ],
+            )
+            w_raw[load] = raw
+
+        def issue_weight_load(turn):
+            if (turn - W_LAG) % W_LOAD == 0 and 0 <= turn - W_LAG < W_PASSES:
+                load_weight((turn - W_LAG) // W_LOAD)
+
+        def turn_weight(w):
+            if w % PAIR == 0:
+                grouped = w_kept.tile([P, PAIR_COLS], BF16, align_bytes=64, name="w_grouped")
+                w_grouped[w // PAIR] = grouped
+            words = w_grouped[w // PAIR][:].bitcast(F32).rearrange(
+                "p (g n o u) -> p g n o u", g=PAIR, n=2, u=2
+            )
+            for n in range(2):
+                w_bank = w_turned.tile([P, BANK], F32)
+                for u in range(2):
+                    for b in range(2):
+                        transpose_words(
+                            nc, w_bank[:, (2 * u + b) * P : (2 * u + b + 1) * P],
+                            w_raw[w // W_LOAD][:, 2 * n + b, :],
+                            (w % W_LOAD) * WORDS, u, ident[:],
+                        )
+                nc.scalar.copy(
+                    out=words[:, w % PAIR, n], in_=w_bank[:].rearrange("p (u o) -> p o u", u=2)
+                )
+
+        with ExitStack() as stage1:
+            once = stage1.enter_context(tc.tile_pool(name="once", bufs=1))
+            mw_in = stage1.enter_context(tc.tile_pool(name="mw_in", bufs=AHEAD + 1))
+            x_in = stage1.enter_context(tc.tile_pool(name="x_in", bufs=3))
+            work = stage1.enter_context(tc.tile_pool(name="work", bufs=3))
+            turned = stage1.enter_context(tc.psum_pool(name="turned", bufs=2))
+            turned_x = stage1.enter_context(tc.psum_pool(name="turned_x", bufs=2))
+            s_psum = stage1.enter_context(tc.psum_pool(name="s_psum", bufs=2))
+
+            x_raw = {}
+            mw_raw = {}
+            mw_grouped = {}
+            mw_codes = {}
+            mw_scales = {}
+            x_banks = {}
+            s_values = {}
+            prod_grouped = {}
+
+            def load_mod_w(g):
+                raw = mw_in.tile([P, 4, MOD_DIM], BF16, name="mw_raw")
+                nc.sync.dma_start(out=raw[:], in_=mod_w_rows[:, g, :, :])
+                mw_raw[g] = raw
+
+            def load_x(load):
+                raw = x_in.tile([P, TOKEN_TILES, X_LOAD * K_PASS], BF16, name="x_raw")
+                nc.sync.dma_start(
+                    out=raw[:],
+                    in_=x_rows[:, :, load * X_LOAD * K_PASS : (load + 1) * X_LOAD * K_PASS],
+                )
+                x_raw[load] = raw
+
+            def issue_loads(turn):
+                if turn < PASSES:
+                    load_mod_w(turn)
+                if (turn - 1) % X_LOAD == 0 and turn - 1 < PASSES:
+                    load_x((turn - 1) // X_LOAD)
+                issue_weight_load(turn)
+
+            def turn_mod_w(g):
+                grouped = work.tile([P, 4 * P * 4], BF16, align_bytes=64, name="mw_grouped")
+                words = grouped[:].bitcast(F32).rearrange("p (u e r v) -> p u e r v", u=2, e=2, v=2)
+                for u in range(2):
+                    mw_bank = turned.tile([P, BANK], F32, tag="bank")
+                    for e in range(2):
+                        for v in range(2):
+                            transpose_words(
+                                nc, mw_bank[:, (2 * e + v) * P : (2 * e + v + 1) * P],
+                                mw_raw[g][:, 2 * u + e, :], 0, v, ident[:],
+                            )
+                    nc.scalar.copy(
+                        out=words[:, u], in_=mw_bank[:].rearrange("p (e v r) -> p e r v", e=2, v=2)
+                    )
+                mw_grouped[g] = grouped
+
+            def quantise_mod_w(g):
+                codes = work.tile([P, 4 * P], U32, align_bytes=64, name="mw_codes")
+                scales = work.tile([P, 4 * P], U8, align_bytes=64, name="mw_scales")
+                nc.vector.quantize_mx(
+                    out=codes[:].bitcast(FP8X4), scales=scales[:], in_=mw_grouped[g][:]
+                )
+                mw_codes[g] = codes
+                mw_scales[g] = scales
+
+            def first_matmul(g):
+                x_bank = turned_x.tile([P, BANK], F32)
+                for u in range(2):
+                    for a in range(TOKEN_TILES):
+                        transpose_words(
+                            nc, x_bank[:, (u * TOKEN_TILES + a) * P : (u * TOKEN_TILES + a + 1) * P],
+                            x_raw[g // X_LOAD][:, a, :], (g % X_LOAD) * WORDS, u, ident[:],
+                        )
+                x_banks[g] = x_bank
+                s_sb = work.tile([P, 4 * TOKENS], F32)
+                s_halves = []
+                for u in range(2):
+                    s_bank = s_psum.tile([P, BANK], F32)
+                    for e in range(2):
+                        j = 2 * u + e
+                        nc.tensor.matmul_mx(
+                            out=s_bank[:, e * TOKENS : (e + 1) * TOKENS],
+                            lhsT=mw_codes[g][:, j * P : (j + 1) * P].bitcast(FP8X4),
+                            lhsT_scale=mw_scales[g][:, j * P : (j + 1) * P],
+                            rhs=mod_codes[:].bitcast(FP8X4),
+                            rhs_scale=mod_scales[:],
+                            start=True,
+                            stop=True,
+                        )
+                    s_halves.append(s_bank)
+                for u in range(2):
+                    nc.vector.tensor_tensor(
+                        out=s_sb[:, u * BANK : (u + 1) * BANK].rearrange("p (t e) -> p t e", e=2),
+                        in0=s_halves[u][:].rearrange("p (e t) -> p t e", e=2),
+                        in1=mod_b_cols[:, 4 * g + 2 * u : 4 * g + 2 * u + 2]
+                        .unsqueeze(1)
+                        .to_broadcast([P, TOKENS, 2]),
+                        op=ALU.add,
+                    )
+                s_values[g] = s_sb
+
+            def products(g):
+                prod = work.tile([P, 2 * TOKENS * 4], BF16, align_bytes=64, name="prod_grouped")
+                s_view = s_values[g][:].rearrange("p (u t e) -> p t u e", u=2, e=2)
+                nc.vector.tensor_tensor(
+                    out=prod[:, : TOKENS * 4].rearrange("p (t u e) -> p t u e", u=2, e=2),
+                    in0=x_banks[g][:].bitcast(BF16).rearrange("p (u t e) -> p t u e", u=2, e=2),
+                    in1=s_view,
+                    op=ALU.mult,
+                )
+                nc.scalar.activation(
+                    out=prod[:, TOKENS * 4 :].rearrange("p (t u e) -> p t u e", u=2, e=2),
+                    in_=s_view,
+                    func=ACT.Square,
+                )
+                prod_grouped[g] = prod
+
+            def quantise_products(g):
+                kept = slice(g * 2 * TOKENS, (g + 1) * 2 * TOKENS)
+                nc.vector.quantize_mx(
+                    out=prod_codes[:, kept].bitcast(FP8X4), scales=prod_scales[:, kept],
+                    in_=prod_grouped[g][:],
+                )
+
+            mod_raw = once.tile([P, TOKEN_TILES, MOD_DIM], BF16)
+            nc.sync.dma_start(out=mod_raw[:], in_=modulation_rows)
+            mod_b_raw = once.tile([P, K_PASS], BF16)
+            nc.vector.memset(mod_b_raw[:], 0.0)
+            nc.sync.dma_start(
+                out=mod_b_raw[:PASSES, :], in_=mod_b.rearrange("(g k) -> g k", k=K_PASS)
+            )
+            for t in range(AHEAD):
+                issue_loads(t)
+
+            mod_bank = turned.tile([P, BANK], F32, tag="bank")
+            for u in range(2):
+                for a in range(TOKEN_TILES):
+                    transpose_words(
+                        nc, mod_bank[:, (u * TOKEN_TILES + a) * P : (u * TOKEN_TILES + a + 1) * P],
+                        mod_raw[:, a, :], 0, u, ident[:],
+                    )
+            mod_grouped = once.tile([P, TOKENS * 4], BF16, align_bytes=64)
+            nc.scalar.copy(
+                out=mod_grouped[:].bitcast(F32).rearrange("p (t u) -> p t u", u=2),
+                in_=mod_bank[:].rearrange("p (u t) -> p t u", u=2),
+            )
+            mod_codes = once.tile([P, TOKENS], U32, align_bytes=64)
+            mod_scales = once.tile([P, TOKENS], U8, align_bytes=64)
+            nc.vector.quantize_mx(
+                out=mod_codes[:].bitcast(FP8X4), scales=mod_scales[:], in_=mod_grouped[:]
+            )
+
+            mod_b_bank = turned.tile([P, BANK], F32, tag="bank")
+            for u in range(2):
+                transpose_words(
+                    nc, mod_b_bank[:, u * P : (u + 1) * P], mod_b_raw[:], 0, u, ident[:]
+                )
+                nc.vector.tensor_copy(
+                    out=mod_b_cols[:].rearrange("p (g u e) -> p g u e", u=2, e=2)[:, :, u, :],
+                    in_=mod_b_bank[:, u * P : u * P + PASSES].bitcast(BF16).rearrange(
+                        "p (g e) -> p g e", e=2
+                    ),
+                )
+
+            for i in range(STAGE1_TURNS):
+                issue_loads(i + AHEAD)
+                if i < PASSES:
+                    turn_mod_w(i)
+                if i >= W_LAG:
+                    turn_weight(i - W_LAG)
+                if 1 <= i <= PASSES:
+                    quantise_mod_w(i - 1)
+                if 3 <= i < PASSES + 3:
+                    quantise_products(i - 3)
+                if 2 <= i < PASSES + 2:
+                    products(i - 2)
+                if 1 <= i <= PASSES:
+                    first_matmul(i - 1)
+
+        with ExitStack() as stage2:
+            w_work = stage2.enter_context(tc.tile_pool(name="w_work", bufs=3, reuse_waits="tile"))
+            tail = stage2.enter_context(tc.tile_pool(name="tail", bufs=2, reuse_waits="tile"))
+            sums = stage2.enter_context(tc.psum_pool(name="sums", bufs=1, reuse_waits="tile"))
+
+            w_squared = {}
+            w_codes = {}
+            w_scales = {}
+            w2_codes = {}
+            w2_scales = {}
+            y_sums = {}
+            q_sums = {}
+
+            def square(pair):
+                squared = w_work.tile([P, PAIR_COLS], BF16, align_bytes=64, name="w_squared")
+                nc.vector.tensor_tensor(
+                    out=squared[:, :SQUARE_COLS_VECTOR],
+                    in0=w_grouped[pair][:, :SQUARE_COLS_VECTOR],
+                    in1=w_grouped[pair][:, :SQUARE_COLS_VECTOR],
+                    op=ALU.mult,
+                )
+                nc.scalar.activation(
+                    out=squared[:, SQUARE_COLS_VECTOR:],
+                    in_=w_grouped[pair][:, SQUARE_COLS_VECTOR:],
+                    func=ACT.Square,
+                )
+                w_squared[pair] = squared
+
+            def quantise(pair):
+                codes2 = w_work.tile([P, PAIR_COLS // 4], U32, align_bytes=64, name="w2_codes")
+                scales2 = w_work.tile([P, PAIR_COLS // 4], U8, align_bytes=64, name="w2_scales")
+                nc.vector.quantize_mx(
+                    out=codes2[:].bitcast(FP8X4), scales=scales2[:], in_=w_squared[pair][:]
+                )
+                codes = w_work.tile([P, PAIR_COLS // 4], U32, align_bytes=64, name="w_codes")
+                scales = w_work.tile([P, PAIR_COLS // 4], U8, align_bytes=64, name="w_scales")
+                nc.vector.quantize_mx(
+                    out=codes[:].bitcast(FP8X4), scales=scales[:], in_=w_grouped[pair][:]
+                )
+                w_codes[pair] = codes
+                w_scales[pair] = scales
+                w2_codes[pair] = codes2
+                w2_scales[pair] = scales2
+
+            def multiply_into(banks, product, moving_codes, moving_scales, pair):
+                for gl in range(PAIR):
+                    g = (pair * PAIR + gl) % PASSES
+                    moving = slice(gl * ROUND_OUT, (gl + 1) * ROUND_OUT)
+                    for a in range(TOKEN_TILES):
+                        first = (2 * g + product) * TOKENS + a * P
+                        nc.tensor.matmul_mx(
+                            out=banks[a][:],
+                            lhsT=prod_codes[:, first : first + P].bitcast(FP8X4),
+                            lhsT_scale=prod_scales[:, first : first + P],
+                            rhs=moving_codes[:, moving].bitcast(FP8X4),
+                            rhs_scale=moving_scales[:, moving],
+                            start=(g == 0),
+                            stop=(g == PASSES - 1),
+                        )
+
+            def multiply(pair):
+                if pair % ROUND_PAIRS == 0:
+                    for a in range(TOKEN_TILES):
+                        y_bank = sums.tile([P, BANK], F32, name="y_bank%d" % a)
+                        q_bank = sums.tile([P, BANK], F32, name="q_bank%d" % a, bufs=2)
+                        y_sums[a] = y_bank
+                        q_sums[a] = q_bank
+                multiply_into(q_sums, 1, w2_codes[pair], w2_scales[pair], pair)
+                multiply_into(y_sums, 0, w_codes[pair], w_scales[pair], pair)
+
+            def finish_round(h):
+                results = []
+                for a in range(TOKEN_TILES):
+                    demod = tail.tile([P, ROUND_OUT], F32)
+                    nc.scalar.activation(
+                        out=demod[:], in_=q_sums[a][:], func=ACT.Abs_reciprocal_sqrt, bias=eps[:]
+                    )
+                    result = tail.tile([P, ROUND_OUT], F32)
+                    nc.vector.tensor_tensor(out=result[:], in0=y_sums[a][:], in1=demod[:], op=ALU.mult)
+                    results.append(result)
+                for a in range(TOKEN_TILES):
+                    nc.vector.tensor_tensor(
+                        out=results[a][:], in0=results[a][:],
+                        in1=bias_all[:, h * ROUND_OUT : (h + 1) * ROUND_OUT], op=ALU.add,
+                    )
+                    nc.sync.dma_start(
+                        out=out_rows[a * P : (a + 1) * P, h * ROUND_OUT : (h + 1) * ROUND_OUT],
+                        in_=results[a][:],
+                    )
+
+            square(0)
+            for b in range(W_PAIRS + 1):
+                issue_weight_load(STAGE1_TURNS + b + AHEAD)
+                if b == ROUND_PAIRS + 1:
+                    finish_round(0)
+                if b + 1 < W_PAIRS:
+                    square(b + 1)
+                if b < W_PAIRS:
+                    quantise(b)
+                if W_EARLY + b < W_PASSES:
+                    turn_weight(W_EARLY + b)
+                if b >= 1:
+                    multiply(b - 1)
+            finish_round(1)

@@ -27,20 +27,23 @@ ROUND_OUT = 512
 ROUNDS = OUT_DIM // ROUND_OUT
 ROW_TILES = ROUND_OUT // P
 W_PASSES = ROUNDS * PASSES
+W_COLS = ROUND_OUT * 4
 
 X_LOAD = 2
 W_LOAD = 2
-AHEAD = 3
-PAIR = 2
-PAIR_COLS = PAIR * ROUND_OUT * 4
-W_PAIRS = W_PASSES // PAIR
-ROUND_PAIRS = PASSES // PAIR
-STAGE1_TURNS = PASSES + 4
-W_LAG = 2
-W_EARLY = STAGE1_TURNS - W_LAG
-KEPT_PAIRS = W_EARLY // PAIR
+AHEAD = 2
+KEPT = 18
 
-SQUARE_COLS_VECTOR = 2176
+C1 = 768
+C2 = 1024
+C3 = 1024
+C4 = 1280
+
+TURNED = (0, 1)
+X_BANKS = (2, 3)
+S_BANKS = (4, 5)
+Y_BANKS = ((6, 7), (2, 3))
+Q_BANKS = ((4, 5), (4, 5))
 
 FLOPS = 2 * TOKENS * (MOD_DIM * IN_DIM + 2 * IN_DIM * OUT_DIM)
 
@@ -62,9 +65,14 @@ def tile_modulatedlinear_k_kernel(tc, x, modulation, weight, bias, mod_w, mod_b,
     with ExitStack() as whole:
         whole.enter_context(tc.manual_schedule())
         const = whole.enter_context(tc.tile_pool(name="const", bufs=1))
-        w_in = whole.enter_context(tc.tile_pool(name="w_in", bufs=3))
-        w_kept = whole.enter_context(tc.tile_pool(name="w_kept", bufs=KEPT_PAIRS))
-        w_turned = whole.enter_context(tc.psum_pool(name="w_turned", bufs=2))
+        w_in = whole.enter_context(tc.tile_pool(name="w_in", bufs=2))
+        w_kept = whole.enter_context(tc.tile_pool(name="w_kept", bufs=KEPT))
+        w_work = whole.enter_context(tc.tile_pool(name="w_work", bufs=3))
+        tail = whole.enter_context(tc.tile_pool(name="tail", bufs=2))
+        psum = whole.enter_context(tc.psum_pool(name="psum", bufs=1))
+
+        def bank(n):
+            return psum.tile([P, BANK], F32, name="bank%d" % n)
 
         ident = const.tile([P, P], F32)
         make_identity(nc, ident[:])
@@ -82,6 +90,13 @@ def tile_modulatedlinear_k_kernel(tc, x, modulation, weight, bias, mod_w, mod_b,
 
         w_raw = {}
         w_grouped = {}
+        w_squared = {}
+        w_quantised = {}
+        w2_quantised = {}
+        y_sums = {}
+        q_sums = {}
+        demods = {}
+        results = {}
 
         def load_weight(load):
             first = load * W_LOAD
@@ -95,19 +110,16 @@ def tile_modulatedlinear_k_kernel(tc, x, modulation, weight, bias, mod_w, mod_b,
             )
             w_raw[load] = raw
 
-        def issue_weight_load(turn):
-            if (turn - W_LAG) % W_LOAD == 0 and 0 <= turn - W_LAG < W_PASSES:
-                load_weight((turn - W_LAG) // W_LOAD)
+        def load_weights_to(w):
+            while len(w_raw) * W_LOAD <= min(w, W_PASSES - 1):
+                load_weight(len(w_raw))
 
         def turn_weight(w):
-            if w % PAIR == 0:
-                grouped = w_kept.tile([P, PAIR_COLS], BF16, align_bytes=64, name="w_grouped")
-                w_grouped[w // PAIR] = grouped
-            words = w_grouped[w // PAIR][:].bitcast(F32).rearrange(
-                "p (g n o u) -> p g n o u", g=PAIR, n=2, u=2
-            )
+            load_weights_to(w + AHEAD)
+            grouped = w_kept.tile([P, W_COLS], BF16, align_bytes=64, name="w_grouped")
+            words = grouped[:].bitcast(F32).rearrange("p (n o u) -> p n o u", n=2, u=2)
             for n in range(2):
-                w_bank = w_turned.tile([P, BANK], F32)
+                w_bank = bank(TURNED[n])
                 for u in range(2):
                     for b in range(2):
                         transpose_words(
@@ -116,17 +128,98 @@ def tile_modulatedlinear_k_kernel(tc, x, modulation, weight, bias, mod_w, mod_b,
                             (w % W_LOAD) * WORDS, u, ident[:],
                         )
                 nc.scalar.copy(
-                    out=words[:, w % PAIR, n], in_=w_bank[:].rearrange("p (u o) -> p o u", u=2)
+                    out=words[:, n], in_=w_bank[:].rearrange("p (u o) -> p o u", u=2)
                 )
+            w_grouped[w] = grouped
+
+        def square_on_scalar(w, first, end):
+            if end > first:
+                cols = w_grouped[w][:, first:end]
+                nc.scalar.activation(out=cols, in_=cols, func=ACT.Square)
+
+        def square_on_vector(w, first, end):
+            if end > first:
+                cols = w_grouped[w][:, first:end]
+                nc.vector.tensor_tensor(out=cols, in0=cols, in1=cols, op=ALU.mult)
+
+        def square_apart(w, pool, scalar_cols):
+            squared = pool.tile([P, W_COLS], BF16, align_bytes=64, name="w_squared")
+            nc.scalar.activation(
+                out=squared[:, :scalar_cols], in_=w_grouped[w][:, :scalar_cols], func=ACT.Square
+            )
+            if scalar_cols < W_COLS:
+                cols = w_grouped[w][:, scalar_cols:]
+                nc.vector.tensor_tensor(
+                    out=squared[:, scalar_cols:], in0=cols, in1=cols, op=ALU.mult
+                )
+            w_squared[w] = squared
+
+        def quantise(values, kind):
+            codes = w_work.tile([P, ROUND_OUT], U32, align_bytes=64, name=kind + "_codes")
+            scales = w_work.tile([P, ROUND_OUT], U8, align_bytes=64, name=kind + "_scales")
+            nc.vector.quantize_mx(
+                out=codes[:].bitcast(FP8X4), scales=scales[:], in_=values[:]
+            )
+            return codes, scales
+
+        def quantise_weight(w):
+            w_quantised[w] = quantise(w_grouped[w], "w")
+
+        def quantise_squares(w):
+            w2_quantised[w] = quantise(w_squared.get(w, w_grouped[w]), "w2")
+
+        def multiply_into(sums, product, moving, w, a):
+            g = w % PASSES
+            first = (2 * g + product) * TOKENS + a * P
+            nc.tensor.matmul_mx(
+                out=sums[a][:],
+                lhsT=prod_codes[:, first : first + P].bitcast(FP8X4),
+                lhsT_scale=prod_scales[:, first : first + P],
+                rhs=moving[0][:].bitcast(FP8X4),
+                rhs_scale=moving[1][:],
+                start=(g == 0),
+                stop=(g == PASSES - 1),
+            )
+
+        def multiply_weight(w, a):
+            if w % PASSES == 0:
+                y_sums[w // PASSES, a] = bank(Y_BANKS[w // PASSES][a])
+            multiply_into({a: y_sums[w // PASSES, a]}, 0, w_quantised[w], w, a)
+
+        def multiply_squares(w, a):
+            if w % PASSES == 0:
+                q_sums[w // PASSES, a] = bank(Q_BANKS[w // PASSES][a])
+            multiply_into({a: q_sums[w // PASSES, a]}, 1, w2_quantised[w], w, a)
+
+        def demodulation(h, a):
+            demod = tail.tile([P, ROUND_OUT], F32, name="demod")
+            nc.scalar.activation(
+                out=demod[:], in_=q_sums[h, a][:], func=ACT.Abs_reciprocal_sqrt, bias=eps[:]
+            )
+            demods[h, a] = demod
+
+        def scale_y(h, a):
+            result = tail.tile([P, ROUND_OUT], F32, name="result")
+            nc.vector.tensor_tensor(
+                out=result[:], in0=y_sums[h, a][:], in1=demods[h, a][:], op=ALU.mult
+            )
+            results[h, a] = result
+
+        def add_bias_and_store(h, a):
+            nc.vector.tensor_tensor(
+                out=results[h, a][:], in0=results[h, a][:],
+                in1=bias_all[:, h * ROUND_OUT : (h + 1) * ROUND_OUT], op=ALU.add,
+            )
+            nc.sync.dma_start(
+                out=out_rows[a * P : (a + 1) * P, h * ROUND_OUT : (h + 1) * ROUND_OUT],
+                in_=results[h, a][:],
+            )
 
         with ExitStack() as stage1:
             once = stage1.enter_context(tc.tile_pool(name="once", bufs=1))
-            mw_in = stage1.enter_context(tc.tile_pool(name="mw_in", bufs=AHEAD + 1))
-            x_in = stage1.enter_context(tc.tile_pool(name="x_in", bufs=3))
+            mw_in = stage1.enter_context(tc.tile_pool(name="mw_in", bufs=3))
+            x_in = stage1.enter_context(tc.tile_pool(name="x_in", bufs=2))
             work = stage1.enter_context(tc.tile_pool(name="work", bufs=3))
-            turned = stage1.enter_context(tc.psum_pool(name="turned", bufs=2))
-            turned_x = stage1.enter_context(tc.psum_pool(name="turned_x", bufs=2))
-            s_psum = stage1.enter_context(tc.psum_pool(name="s_psum", bufs=2))
 
             x_raw = {}
             mw_raw = {}
@@ -134,6 +227,7 @@ def tile_modulatedlinear_k_kernel(tc, x, modulation, weight, bias, mod_w, mod_b,
             mw_codes = {}
             mw_scales = {}
             x_banks = {}
+            s_banks = {}
             s_values = {}
             prod_grouped = {}
 
@@ -150,18 +244,19 @@ def tile_modulatedlinear_k_kernel(tc, x, modulation, weight, bias, mod_w, mod_b,
                 )
                 x_raw[load] = raw
 
-            def issue_loads(turn):
-                if turn < PASSES:
-                    load_mod_w(turn)
-                if (turn - 1) % X_LOAD == 0 and turn - 1 < PASSES:
-                    load_x((turn - 1) // X_LOAD)
-                issue_weight_load(turn)
+            def load_mod_w_to(g):
+                while len(mw_raw) <= min(g, PASSES - 1):
+                    load_mod_w(len(mw_raw))
+
+            def load_x_to(g):
+                while len(x_raw) * X_LOAD <= min(g, PASSES - 1):
+                    load_x(len(x_raw))
 
             def turn_mod_w(g):
-                grouped = work.tile([P, 4 * P * 4], BF16, align_bytes=64, name="mw_grouped")
+                grouped = work.tile([P, 4 * P * 4], BF16, align_bytes=64, name="mw_grouped", bufs=2)
                 words = grouped[:].bitcast(F32).rearrange("p (u e r v) -> p u e r v", u=2, e=2, v=2)
                 for u in range(2):
-                    mw_bank = turned.tile([P, BANK], F32, tag="bank")
+                    mw_bank = bank(TURNED[u])
                     for e in range(2):
                         for v in range(2):
                             transpose_words(
@@ -174,65 +269,67 @@ def tile_modulatedlinear_k_kernel(tc, x, modulation, weight, bias, mod_w, mod_b,
                 mw_grouped[g] = grouped
 
             def quantise_mod_w(g):
-                codes = work.tile([P, 4 * P], U32, align_bytes=64, name="mw_codes")
-                scales = work.tile([P, 4 * P], U8, align_bytes=64, name="mw_scales")
+                codes = work.tile([P, 4 * P], U32, align_bytes=64, name="mw_codes", bufs=2)
+                scales = work.tile([P, 4 * P], U8, align_bytes=64, name="mw_scales", bufs=2)
                 nc.vector.quantize_mx(
                     out=codes[:].bitcast(FP8X4), scales=scales[:], in_=mw_grouped[g][:]
                 )
                 mw_codes[g] = codes
                 mw_scales[g] = scales
 
-            def first_matmul(g):
-                x_bank = turned_x.tile([P, BANK], F32)
-                for u in range(2):
-                    for a in range(TOKEN_TILES):
-                        transpose_words(
-                            nc, x_bank[:, (u * TOKEN_TILES + a) * P : (u * TOKEN_TILES + a + 1) * P],
-                            x_raw[g // X_LOAD][:, a, :], (g % X_LOAD) * WORDS, u, ident[:],
-                        )
-                x_banks[g] = x_bank
-                s_sb = work.tile([P, 4 * TOKENS], F32)
-                s_halves = []
-                for u in range(2):
-                    s_bank = s_psum.tile([P, BANK], F32)
-                    for e in range(2):
-                        j = 2 * u + e
-                        nc.tensor.matmul_mx(
-                            out=s_bank[:, e * TOKENS : (e + 1) * TOKENS],
-                            lhsT=mw_codes[g][:, j * P : (j + 1) * P].bitcast(FP8X4),
-                            lhsT_scale=mw_scales[g][:, j * P : (j + 1) * P],
-                            rhs=mod_codes[:].bitcast(FP8X4),
-                            rhs_scale=mod_scales[:],
-                            start=True,
-                            stop=True,
-                        )
-                    s_halves.append(s_bank)
-                for u in range(2):
-                    nc.vector.tensor_tensor(
-                        out=s_sb[:, u * BANK : (u + 1) * BANK].rearrange("p (t e) -> p t e", e=2),
-                        in0=s_halves[u][:].rearrange("p (e t) -> p t e", e=2),
-                        in1=mod_b_cols[:, 4 * g + 2 * u : 4 * g + 2 * u + 2]
-                        .unsqueeze(1)
-                        .to_broadcast([P, TOKENS, 2]),
-                        op=ALU.add,
+            def turn_x(g, u):
+                if u == 0:
+                    x_banks[g] = bank(X_BANKS[g % 2])
+                for a in range(TOKEN_TILES):
+                    transpose_words(
+                        nc, x_banks[g][:, (u * TOKEN_TILES + a) * P : (u * TOKEN_TILES + a + 1) * P],
+                        x_raw[g // X_LOAD][:, a, :], (g % X_LOAD) * WORDS, u, ident[:],
                     )
-                s_values[g] = s_sb
 
-            def products(g):
+            def first_matmul(g, u):
+                s_bank = bank(S_BANKS[u])
+                for e in range(2):
+                    j = 2 * u + e
+                    nc.tensor.matmul_mx(
+                        out=s_bank[:, e * TOKENS : (e + 1) * TOKENS],
+                        lhsT=mw_codes[g][:, j * P : (j + 1) * P].bitcast(FP8X4),
+                        lhsT_scale=mw_scales[g][:, j * P : (j + 1) * P],
+                        rhs=mod_codes[:].bitcast(FP8X4),
+                        rhs_scale=mod_scales[:],
+                        start=True,
+                        stop=True,
+                    )
+                s_banks[g, u] = s_bank
+
+            def add_mod_b(g, u):
+                if u == 0:
+                    s_sb = work.tile([P, 4 * TOKENS], F32, name="s_sb")
+                    s_values[g] = s_sb
+                nc.vector.tensor_tensor(
+                    out=s_values[g][:, u * BANK : (u + 1) * BANK].rearrange("p (t e) -> p t e", e=2),
+                    in0=s_banks[g, u][:].rearrange("p (e t) -> p t e", e=2),
+                    in1=mod_b_cols[:, 4 * g + 2 * u : 4 * g + 2 * u + 2]
+                    .unsqueeze(1)
+                    .to_broadcast([P, TOKENS, 2]),
+                    op=ALU.add,
+                )
+
+            def multiply_x(g):
                 prod = work.tile([P, 2 * TOKENS * 4], BF16, align_bytes=64, name="prod_grouped")
-                s_view = s_values[g][:].rearrange("p (u t e) -> p t u e", u=2, e=2)
+                prod_grouped[g] = prod
                 nc.vector.tensor_tensor(
                     out=prod[:, : TOKENS * 4].rearrange("p (t u e) -> p t u e", u=2, e=2),
                     in0=x_banks[g][:].bitcast(BF16).rearrange("p (u t e) -> p t u e", u=2, e=2),
-                    in1=s_view,
+                    in1=s_values[g][:].rearrange("p (u t e) -> p t u e", u=2, e=2),
                     op=ALU.mult,
                 )
+
+            def square_s(g):
                 nc.scalar.activation(
-                    out=prod[:, TOKENS * 4 :].rearrange("p (t u e) -> p t u e", u=2, e=2),
-                    in_=s_view,
+                    out=prod_grouped[g][:, TOKENS * 4 :].rearrange("p (t u e) -> p t u e", u=2, e=2),
+                    in_=s_values[g][:].rearrange("p (u t e) -> p t u e", u=2, e=2),
                     func=ACT.Square,
                 )
-                prod_grouped[g] = prod
 
             def quantise_products(g):
                 kept = slice(g * 2 * TOKENS, (g + 1) * 2 * TOKENS)
@@ -245,13 +342,16 @@ def tile_modulatedlinear_k_kernel(tc, x, modulation, weight, bias, mod_w, mod_b,
             nc.sync.dma_start(out=mod_raw[:], in_=modulation_rows)
             mod_b_raw = once.tile([P, K_PASS], BF16)
             nc.vector.memset(mod_b_raw[:], 0.0)
+            load_mod_w_to(0)
             nc.sync.dma_start(
                 out=mod_b_raw[:PASSES, :], in_=mod_b.rearrange("(g k) -> g k", k=K_PASS)
             )
-            for t in range(AHEAD):
-                issue_loads(t)
+            load_mod_w_to(1)
+            load_x_to(0)
+            load_weights_to(0)
+            load_mod_w_to(2)
 
-            mod_bank = turned.tile([P, BANK], F32, tag="bank")
+            mod_bank = bank(6)
             for u in range(2):
                 for a in range(TOKEN_TILES):
                     transpose_words(
@@ -259,7 +359,7 @@ def tile_modulatedlinear_k_kernel(tc, x, modulation, weight, bias, mod_w, mod_b,
                         mod_raw[:, a, :], 0, u, ident[:],
                     )
             mod_grouped = once.tile([P, TOKENS * 4], BF16, align_bytes=64)
-            nc.scalar.copy(
+            nc.vector.tensor_copy(
                 out=mod_grouped[:].bitcast(F32).rearrange("p (t u) -> p t u", u=2),
                 in_=mod_bank[:].rearrange("p (u t) -> p t u", u=2),
             )
@@ -269,134 +369,127 @@ def tile_modulatedlinear_k_kernel(tc, x, modulation, weight, bias, mod_w, mod_b,
                 out=mod_codes[:].bitcast(FP8X4), scales=mod_scales[:], in_=mod_grouped[:]
             )
 
-            mod_b_bank = turned.tile([P, BANK], F32, tag="bank")
-            for u in range(2):
-                transpose_words(
-                    nc, mod_b_bank[:, u * P : (u + 1) * P], mod_b_raw[:], 0, u, ident[:]
-                )
-                nc.vector.tensor_copy(
-                    out=mod_b_cols[:].rearrange("p (g u e) -> p g u e", u=2, e=2)[:, :, u, :],
-                    in_=mod_b_bank[:, u * P : u * P + PASSES].bitcast(BF16).rearrange(
-                        "p (g e) -> p g e", e=2
-                    ),
-                )
+            def turn_mod_b():
+                mod_b_bank = bank(7)
+                for u in range(2):
+                    transpose_words(
+                        nc, mod_b_bank[:, u * P : (u + 1) * P], mod_b_raw[:], 0, u, ident[:]
+                    )
+                for u in range(2):
+                    nc.vector.tensor_copy(
+                        out=mod_b_cols[:].rearrange("p (g u e) -> p g u e", u=2, e=2)[:, :, u, :],
+                        in_=mod_b_bank[:, u * P : u * P + PASSES].bitcast(BF16).rearrange(
+                            "p (g e) -> p g e", e=2
+                        ),
+                    )
 
-            for i in range(STAGE1_TURNS):
-                issue_loads(i + AHEAD)
+            for i in range(PASSES + 1):
+                load_mod_w_to(i + AHEAD)
+                load_x_to(i - 1 + AHEAD)
                 if i < PASSES:
                     turn_mod_w(i)
-                if i >= W_LAG:
-                    turn_weight(i - W_LAG)
-                if 1 <= i <= PASSES:
-                    quantise_mod_w(i - 1)
-                if 3 <= i < PASSES + 3:
-                    quantise_products(i - 3)
-                if 2 <= i < PASSES + 2:
-                    products(i - 2)
-                if 1 <= i <= PASSES:
-                    first_matmul(i - 1)
+                if i == 0:
+                    turn_mod_b()
+                if i >= 2:
+                    add_mod_b(i - 2, 1)
+                if i >= 1:
+                    turn_x(i - 1, 0)
+                    first_matmul(i - 1, 0)
+                if i >= 3:
+                    multiply_weight(i - 3, 0)
+                if i >= 2:
+                    quantise_weight(i - 2)
+                    multiply_x(i - 2)
+                    square_s(i - 2)
+                if i >= 1:
+                    turn_weight(i - 1)
+                    turn_x(i - 1, 1)
+                    add_mod_b(i - 1, 0)
+                    first_matmul(i - 1, 1)
+                if i >= 3:
+                    multiply_weight(i - 3, 1)
+                if i < PASSES:
+                    quantise_mod_w(i)
+                if i >= 2:
+                    quantise_products(i - 2)
+                    square_on_scalar(i - 2, 0, C1)
+            square_on_scalar(0, C1, C2)
+            square_on_vector(0, C2, W_COLS)
+            add_mod_b(PASSES - 1, 1)
+            quantise_weight(PASSES - 1)
+            multiply_x(PASSES - 1)
+            quantise_squares(0)
+            turn_weight(PASSES)
+            square_s(PASSES - 1)
+            square_on_scalar(PASSES - 1, 0, C1)
+            square_on_scalar(1, C1, C2)
+            square_on_vector(1, C2, W_COLS)
+            for a in range(TOKEN_TILES):
+                multiply_weight(PASSES - 2, a)
+            for a in range(TOKEN_TILES):
+                multiply_squares(0, a)
+            quantise_squares(1)
+            quantise_products(PASSES - 1)
+            for q in (2, 3):
+                square_on_scalar(q, C1, C2)
+                square_on_vector(q, C2, W_COLS)
 
-        with ExitStack() as stage2:
-            w_work = stage2.enter_context(tc.tile_pool(name="w_work", bufs=3, reuse_waits="tile"))
-            tail = stage2.enter_context(tc.tile_pool(name="tail", bufs=2, reuse_waits="tile"))
-            sums = stage2.enter_context(tc.psum_pool(name="sums", bufs=1, reuse_waits="tile"))
-
-            w_squared = {}
-            w_codes = {}
-            w_scales = {}
-            w2_codes = {}
-            w2_scales = {}
-            y_sums = {}
-            q_sums = {}
-
-            def square(pair):
-                squared = w_work.tile([P, PAIR_COLS], BF16, align_bytes=64, name="w_squared")
-                nc.vector.tensor_tensor(
-                    out=squared[:, :SQUARE_COLS_VECTOR],
-                    in0=w_grouped[pair][:, :SQUARE_COLS_VECTOR],
-                    in1=w_grouped[pair][:, :SQUARE_COLS_VECTOR],
-                    op=ALU.mult,
-                )
-                nc.scalar.activation(
-                    out=squared[:, SQUARE_COLS_VECTOR:],
-                    in_=w_grouped[pair][:, SQUARE_COLS_VECTOR:],
-                    func=ACT.Square,
-                )
-                w_squared[pair] = squared
-
-            def quantise(pair):
-                codes2 = w_work.tile([P, PAIR_COLS // 4], U32, align_bytes=64, name="w2_codes")
-                scales2 = w_work.tile([P, PAIR_COLS // 4], U8, align_bytes=64, name="w2_scales")
-                nc.vector.quantize_mx(
-                    out=codes2[:].bitcast(FP8X4), scales=scales2[:], in_=w_squared[pair][:]
-                )
-                codes = w_work.tile([P, PAIR_COLS // 4], U32, align_bytes=64, name="w_codes")
-                scales = w_work.tile([P, PAIR_COLS // 4], U8, align_bytes=64, name="w_scales")
-                nc.vector.quantize_mx(
-                    out=codes[:].bitcast(FP8X4), scales=scales[:], in_=w_grouped[pair][:]
-                )
-                w_codes[pair] = codes
-                w_scales[pair] = scales
-                w2_codes[pair] = codes2
-                w2_scales[pair] = scales2
-
-            def multiply_into(banks, product, moving_codes, moving_scales, pair):
-                for gl in range(PAIR):
-                    g = (pair * PAIR + gl) % PASSES
-                    moving = slice(gl * ROUND_OUT, (gl + 1) * ROUND_OUT)
-                    for a in range(TOKEN_TILES):
-                        first = (2 * g + product) * TOKENS + a * P
-                        nc.tensor.matmul_mx(
-                            out=banks[a][:],
-                            lhsT=prod_codes[:, first : first + P].bitcast(FP8X4),
-                            lhsT_scale=prod_scales[:, first : first + P],
-                            rhs=moving_codes[:, moving].bitcast(FP8X4),
-                            rhs_scale=moving_scales[:, moving],
-                            start=(g == 0),
-                            stop=(g == PASSES - 1),
-                        )
-
-            def multiply(pair):
-                if pair % ROUND_PAIRS == 0:
-                    for a in range(TOKEN_TILES):
-                        y_bank = sums.tile([P, BANK], F32, name="y_bank%d" % a)
-                        q_bank = sums.tile([P, BANK], F32, name="q_bank%d" % a, bufs=2)
-                        y_sums[a] = y_bank
-                        q_sums[a] = q_bank
-                multiply_into(q_sums, 1, w2_codes[pair], w2_scales[pair], pair)
-                multiply_into(y_sums, 0, w_codes[pair], w_scales[pair], pair)
-
-            def finish_round(h):
-                results = []
+        sq_pool = whole.enter_context(tc.tile_pool(name="w_sq", bufs=6))
+        nsq = PASSES
+        for c in range(1, PASSES):
+            turn_weight(PASSES + c)
+            if c == 1:
                 for a in range(TOKEN_TILES):
-                    demod = tail.tile([P, ROUND_OUT], F32)
-                    nc.scalar.activation(
-                        out=demod[:], in_=q_sums[a][:], func=ACT.Abs_reciprocal_sqrt, bias=eps[:]
-                    )
-                    result = tail.tile([P, ROUND_OUT], F32)
-                    nc.vector.tensor_tensor(out=result[:], in0=y_sums[a][:], in1=demod[:], op=ALU.mult)
-                    results.append(result)
+                    multiply_weight(PASSES - 1, a)
                 for a in range(TOKEN_TILES):
-                    nc.vector.tensor_tensor(
-                        out=results[a][:], in0=results[a][:],
-                        in1=bias_all[:, h * ROUND_OUT : (h + 1) * ROUND_OUT], op=ALU.add,
-                    )
-                    nc.sync.dma_start(
-                        out=out_rows[a * P : (a + 1) * P, h * ROUND_OUT : (h + 1) * ROUND_OUT],
-                        in_=results[a][:],
-                    )
+                    multiply_squares(1, a)
+            elif c <= 8:
+                for q in (2 * c - 2, 2 * c - 1):
+                    for a in range(TOKEN_TILES):
+                        multiply_squares(q, a)
+            else:
+                for a in range(TOKEN_TILES):
+                    multiply_squares(c + 7, a)
+                for a in range(TOKEN_TILES):
+                    multiply_weight(c + 7, a)
+            if c == 8:
+                for a in range(TOKEN_TILES):
+                    demodulation(0, a)
+            if c <= 7:
+                for q in (2 * c, 2 * c + 1):
+                    quantise_squares(q)
+            else:
+                quantise_squares(c + 8)
+                quantise_weight(c + 8)
+            if c == 9:
+                for a in range(TOKEN_TILES):
+                    scale_y(0, a)
+            if c == 10:
+                for a in range(TOKEN_TILES):
+                    add_bias_and_store(0, a)
+            if c <= 6:
+                for q in (2 * c + 2, 2 * c + 3):
+                    square_on_scalar(q, C1, C2)
+                    square_on_vector(q, C2, W_COLS)
+            if c >= 5:
+                square_apart(nsq, sq_pool, C3)
+                nsq += 1
 
-            square(0)
-            for b in range(W_PAIRS + 1):
-                issue_weight_load(STAGE1_TURNS + b + AHEAD)
-                if b == ROUND_PAIRS + 1:
-                    finish_round(0)
-                if b + 1 < W_PAIRS:
-                    square(b + 1)
-                if b < W_PAIRS:
-                    quantise(b)
-                if W_EARLY + b < W_PASSES:
-                    turn_weight(W_EARLY + b)
-                if b >= 1:
-                    multiply(b - 1)
-            finish_round(1)
+        for w in range(PASSES + 7, W_PASSES):
+            for a in range(TOKEN_TILES):
+                multiply_squares(w, a)
+            if w == W_PASSES - 1:
+                for a in range(TOKEN_TILES):
+                    demodulation(1, a)
+            for a in range(TOKEN_TILES):
+                multiply_weight(w, a)
+            if w + 1 < W_PASSES:
+                quantise_squares(w + 1)
+                quantise_weight(w + 1)
+            if nsq < W_PASSES:
+                square_apart(nsq, sq_pool, C4)
+                nsq += 1
+        for a in range(TOKEN_TILES):
+            scale_y(1, a)
+        for a in range(TOKEN_TILES):
+            add_bias_and_store(1, a)

@@ -31,7 +31,7 @@ W_COLS = ROUND_OUT * 4
 
 X_LOAD = 2
 W_LOAD = 2
-AHEAD = 2
+AHEAD = 3
 KEPT = 18
 
 C1 = 768
@@ -65,7 +65,7 @@ def tile_modulatedlinear_k_kernel(tc, x, modulation, weight, bias, mod_w, mod_b,
     with ExitStack() as whole:
         whole.enter_context(tc.manual_schedule())
         const = whole.enter_context(tc.tile_pool(name="const", bufs=1))
-        w_in = whole.enter_context(tc.tile_pool(name="w_in", bufs=2))
+        w_in = whole.enter_context(tc.tile_pool(name="w_in", bufs=3))
         w_kept = whole.enter_context(tc.tile_pool(name="w_kept", bufs=KEPT))
         w_work = whole.enter_context(tc.tile_pool(name="w_work", bufs=3))
         tail = whole.enter_context(tc.tile_pool(name="tail", bufs=2))
@@ -217,8 +217,8 @@ def tile_modulatedlinear_k_kernel(tc, x, modulation, weight, bias, mod_w, mod_b,
 
         with ExitStack() as stage1:
             once = stage1.enter_context(tc.tile_pool(name="once", bufs=1))
-            mw_in = stage1.enter_context(tc.tile_pool(name="mw_in", bufs=3))
-            x_in = stage1.enter_context(tc.tile_pool(name="x_in", bufs=2))
+            mw_in = stage1.enter_context(tc.tile_pool(name="mw_in", bufs=4))
+            x_in = stage1.enter_context(tc.tile_pool(name="x_in", bufs=3))
             work = stage1.enter_context(tc.tile_pool(name="work", bufs=3))
 
             x_raw = {}

@@ -31,13 +31,15 @@ W_COLS = ROUND_OUT * 4
 
 X_LOAD = 2
 W_LOAD = 2
-AHEAD = 3
-KEPT = 18
+AHEAD = 2
+KEPT = 17
 
-C1 = 768
-C2 = 1024
-C3 = 1024
-C4 = 1280
+UNITS = 3
+
+C0 = 640
+C1 = 1344
+C2 = 1728
+C3 = 896
 
 TURNED = (0, 1)
 X_BANKS = (2, 3)
@@ -82,7 +84,6 @@ def tile_modulatedlinear_k_kernel(tc, x, modulation, weight, bias, mod_w, mod_b,
         nc.scalar.activation(out=table_warm[:], in_=eps[:], func=ACT.Abs_reciprocal_sqrt)
 
         bias_all = const.tile([P, OUT_DIM], BF16)
-        nc.gpsimd.dma_start(out=bias_all[:], in_=bias.partition_broadcast(P))
 
         prod_codes = const.tile([P, PASSES * 2 * TOKENS], U32, align_bytes=64)
         prod_scales = const.tile([P, PASSES * 2 * TOKENS], U8, align_bytes=64)
@@ -90,7 +91,6 @@ def tile_modulatedlinear_k_kernel(tc, x, modulation, weight, bias, mod_w, mod_b,
 
         w_raw = {}
         w_grouped = {}
-        w_squared = {}
         w_quantised = {}
         w2_quantised = {}
         y_sums = {}
@@ -142,31 +142,19 @@ def tile_modulatedlinear_k_kernel(tc, x, modulation, weight, bias, mod_w, mod_b,
                 cols = w_grouped[w][:, first:end]
                 nc.vector.tensor_tensor(out=cols, in0=cols, in1=cols, op=ALU.mult)
 
-        def square_apart(w, pool, scalar_cols):
-            squared = pool.tile([P, W_COLS], BF16, align_bytes=64, name="w_squared")
-            nc.scalar.activation(
-                out=squared[:, :scalar_cols], in_=w_grouped[w][:, :scalar_cols], func=ACT.Square
-            )
-            if scalar_cols < W_COLS:
-                cols = w_grouped[w][:, scalar_cols:]
-                nc.vector.tensor_tensor(
-                    out=squared[:, scalar_cols:], in0=cols, in1=cols, op=ALU.mult
-                )
-            w_squared[w] = squared
-
-        def quantise(values, kind):
-            codes = w_work.tile([P, ROUND_OUT], U32, align_bytes=64, name=kind + "_codes")
-            scales = w_work.tile([P, ROUND_OUT], U8, align_bytes=64, name=kind + "_scales")
+        def quantise(values, kind, bufs):
+            codes = w_work.tile([P, ROUND_OUT], U32, align_bytes=64, name=kind + "_codes", bufs=bufs)
+            scales = w_work.tile([P, ROUND_OUT], U8, align_bytes=64, name=kind + "_scales", bufs=bufs)
             nc.vector.quantize_mx(
                 out=codes[:].bitcast(FP8X4), scales=scales[:], in_=values[:]
             )
             return codes, scales
 
         def quantise_weight(w):
-            w_quantised[w] = quantise(w_grouped[w], "w")
+            w_quantised[w] = quantise(w_grouped[w], "w", 6)
 
         def quantise_squares(w):
-            w2_quantised[w] = quantise(w_squared.get(w, w_grouped[w]), "w2")
+            w2_quantised[w] = quantise(w_grouped[w], "w2", 6)
 
         def multiply_into(sums, product, moving, w, a):
             g = w % PASSES
@@ -205,11 +193,13 @@ def tile_modulatedlinear_k_kernel(tc, x, modulation, weight, bias, mod_w, mod_b,
             )
             results[h, a] = result
 
-        def add_bias_and_store(h, a):
+        def add_bias(h, a):
             nc.vector.tensor_tensor(
                 out=results[h, a][:], in0=results[h, a][:],
                 in1=bias_all[:, h * ROUND_OUT : (h + 1) * ROUND_OUT], op=ALU.add,
             )
+
+        def store(h, a):
             nc.sync.dma_start(
                 out=out_rows[a * P : (a + 1) * P, h * ROUND_OUT : (h + 1) * ROUND_OUT],
                 in_=results[h, a][:],
@@ -217,7 +207,7 @@ def tile_modulatedlinear_k_kernel(tc, x, modulation, weight, bias, mod_w, mod_b,
 
         with ExitStack() as stage1:
             once = stage1.enter_context(tc.tile_pool(name="once", bufs=1))
-            mw_in = stage1.enter_context(tc.tile_pool(name="mw_in", bufs=4))
+            mw_in = stage1.enter_context(tc.tile_pool(name="mw_in", bufs=3))
             x_in = stage1.enter_context(tc.tile_pool(name="x_in", bufs=3))
             work = stage1.enter_context(tc.tile_pool(name="work", bufs=3))
 
@@ -303,7 +293,7 @@ def tile_modulatedlinear_k_kernel(tc, x, modulation, weight, bias, mod_w, mod_b,
 
             def add_mod_b(g, u):
                 if u == 0:
-                    s_sb = work.tile([P, 4 * TOKENS], F32, name="s_sb")
+                    s_sb = work.tile([P, 4 * TOKENS], F32, name="s_sb", bufs=4)
                     s_values[g] = s_sb
                 nc.vector.tensor_tensor(
                     out=s_values[g][:, u * BANK : (u + 1) * BANK].rearrange("p (t e) -> p t e", e=2),
@@ -315,7 +305,7 @@ def tile_modulatedlinear_k_kernel(tc, x, modulation, weight, bias, mod_w, mod_b,
                 )
 
             def multiply_x(g):
-                prod = work.tile([P, 2 * TOKENS * 4], BF16, align_bytes=64, name="prod_grouped")
+                prod = work.tile([P, 2 * TOKENS * 4], BF16, align_bytes=64, name="prod_grouped", bufs=1)
                 prod_grouped[g] = prod
                 nc.vector.tensor_tensor(
                     out=prod[:, : TOKENS * 4].rearrange("p (t u e) -> p t u e", u=2, e=2),
@@ -325,11 +315,14 @@ def tile_modulatedlinear_k_kernel(tc, x, modulation, weight, bias, mod_w, mod_b,
                 )
 
             def square_s(g):
-                nc.scalar.activation(
-                    out=prod_grouped[g][:, TOKENS * 4 :].rearrange("p (t u e) -> p t u e", u=2, e=2),
-                    in_=s_values[g][:].rearrange("p (u t e) -> p t u e", u=2, e=2),
-                    func=ACT.Square,
+                s_view = s_values[g][:].rearrange("p (u t e) -> p t u e", u=2, e=2)
+                squares = prod_grouped[g][:, TOKENS * 4 :].rearrange(
+                    "p (t u e) -> p t u e", u=2, e=2
                 )
+                if g < PASSES - 1:
+                    nc.gpsimd.tensor_tensor(out=squares, in0=s_view, in1=s_view, op=ALU.mult)
+                else:
+                    nc.scalar.activation(out=squares, in_=s_view, func=ACT.Square)
 
             def quantise_products(g):
                 kept = slice(g * 2 * TOKENS, (g + 1) * 2 * TOKENS)
@@ -386,110 +379,125 @@ def tile_modulatedlinear_k_kernel(tc, x, modulation, weight, bias, mod_w, mod_b,
             for i in range(PASSES + 1):
                 load_mod_w_to(i + AHEAD)
                 load_x_to(i - 1 + AHEAD)
+                if i == 6:
+                    nc.sync.dma_start(out=bias_all[:], in_=bias.partition_broadcast(P))
                 if i < PASSES:
                     turn_mod_w(i)
                 if i == 0:
                     turn_mod_b()
+                if i >= 4:
+                    quantise_products(i - 4)
+                if i >= 3:
+                    quantise_weight(i - 3)
+                    multiply_x(i - 3)
+                    square_s(i - 3)
+                    square_on_scalar(i - 3, 0, C0)
                 if i >= 2:
                     add_mod_b(i - 2, 1)
+                    turn_x(i - 2, 1)
                 if i >= 1:
-                    turn_x(i - 1, 0)
                     first_matmul(i - 1, 0)
-                if i >= 3:
-                    multiply_weight(i - 3, 0)
-                if i >= 2:
-                    quantise_weight(i - 2)
-                    multiply_x(i - 2)
-                    square_s(i - 2)
+                if i >= 4:
+                    multiply_weight(i - 4, 0)
                 if i >= 1:
                     turn_weight(i - 1)
-                    turn_x(i - 1, 1)
+                    turn_x(i - 1, 0)
                     add_mod_b(i - 1, 0)
                     first_matmul(i - 1, 1)
-                if i >= 3:
-                    multiply_weight(i - 3, 1)
+                if i >= 4:
+                    multiply_weight(i - 4, 1)
                 if i < PASSES:
                     quantise_mod_w(i)
-                if i >= 2:
-                    quantise_products(i - 2)
-                    square_on_scalar(i - 2, 0, C1)
-            square_on_scalar(0, C1, C2)
-            square_on_vector(0, C2, W_COLS)
-            add_mod_b(PASSES - 1, 1)
-            quantise_weight(PASSES - 1)
-            multiply_x(PASSES - 1)
-            quantise_squares(0)
+                if i >= 3:
+                    square_on_scalar(i - 3, C0, C1)
+
+            square_on_vector(0, C1, W_COLS)
             turn_weight(PASSES)
-            square_s(PASSES - 1)
-            square_on_scalar(PASSES - 1, 0, C1)
-            square_on_scalar(1, C1, C2)
-            square_on_vector(1, C2, W_COLS)
+            turn_x(PASSES - 1, 1)
+            quantise_products(PASSES - 3)
+            quantise_weight(PASSES - 2)
+            multiply_x(PASSES - 2)
+            square_s(PASSES - 2)
+            add_mod_b(PASSES - 1, 1)
+            square_on_scalar(PASSES - 2, 0, C1)
             for a in range(TOKEN_TILES):
-                multiply_weight(PASSES - 2, a)
+                multiply_weight(PASSES - 3, a)
+            quantise_squares(0)
+            square_on_vector(1, C1, W_COLS)
+
+            turn_weight(PASSES + 1)
+            quantise_products(PASSES - 2)
+            multiply_x(PASSES - 1)
+            square_s(PASSES - 1)
             for a in range(TOKEN_TILES):
                 multiply_squares(0, a)
+            quantise_weight(PASSES - 1)
+            square_on_scalar(PASSES - 1, 0, C1)
             quantise_squares(1)
-            quantise_products(PASSES - 1)
             for q in (2, 3):
-                square_on_scalar(q, C1, C2)
-                square_on_vector(q, C2, W_COLS)
+                square_on_vector(q, C1, W_COLS)
+            for a in range(TOKEN_TILES):
+                multiply_weight(PASSES - 2, a)
 
-        sq_pool = whole.enter_context(tc.tile_pool(name="w_sq", bufs=6))
-        nsq = PASSES
-        for c in range(1, PASSES):
-            turn_weight(PASSES + c)
-            if c == 1:
+            turn_weight(PASSES + 2)
+            quantise_products(PASSES - 1)
+            for a in range(TOKEN_TILES):
+                multiply_squares(1, a)
+            for q in (2, 3, 4):
+                quantise_squares(q)
+                square_on_vector(q + 2, C1, W_COLS)
+            for a in range(TOKEN_TILES):
+                multiply_weight(PASSES - 1, a)
+
+        late_y = list(range(PASSES, W_PASSES))
+        late_q = list(range(PASSES, W_PASSES))
+        quantised = [("q", w) for w in range(5, PASSES)]
+        multiplied = [("q", w) for w in range(2, PASSES)]
+        for k in range(W_PASSES - PASSES + 2):
+            if k < len(late_y):
+                quantised.append(("y", late_y[k]))
+            if k >= 2:
+                quantised.append(("q", late_q[k - 2]))
+        multiplied += [u for u in quantised if u[1] >= PASSES and not (u[0] == "y" and u[1] >= W_PASSES - 2)]
+        multiplied += [("y", W_PASSES - 2), ("y", W_PASSES - 1)]
+        turned = PASSES + 3
+        m = 0
+        v = 0
+        finish_at = {}
+        c = 0
+        while m < len(multiplied):
+            if turned < W_PASSES:
+                turn_weight(turned)
+                turned += 1
+            for kind, w in quantised[v : v + UNITS]:
+                if kind == "q":
+                    quantise_squares(w)
+                    if w + 2 < PASSES:
+                        square_on_scalar(w + 2, C1, C2)
+                        square_on_vector(w + 2, C2, W_COLS)
+                else:
+                    quantise_weight(w)
+                    square_on_scalar(w, 0, C3)
+                    square_on_vector(w, C3, W_COLS)
+            v += UNITS
+            for kind, w in multiplied[m : m + UNITS]:
                 for a in range(TOKEN_TILES):
-                    multiply_weight(PASSES - 1, a)
-                for a in range(TOKEN_TILES):
-                    multiply_squares(1, a)
-            elif c <= 8:
-                for q in (2 * c - 2, 2 * c - 1):
+                    (multiply_squares if kind == "q" else multiply_weight)(w, a)
+                if kind == "q" and w % PASSES == PASSES - 1:
                     for a in range(TOKEN_TILES):
-                        multiply_squares(q, a)
-            else:
+                        demodulation(w // PASSES, a)
+                    if w < PASSES:
+                        finish_at = {c + 1: scale_y, c + 2: add_bias}
+            m += UNITS
+            if c in finish_at:
                 for a in range(TOKEN_TILES):
-                    multiply_squares(c + 7, a)
+                    finish_at[c](0, a)
+            if turned == W_PASSES - 2:
                 for a in range(TOKEN_TILES):
-                    multiply_weight(c + 7, a)
-            if c == 8:
-                for a in range(TOKEN_TILES):
-                    demodulation(0, a)
-            if c <= 7:
-                for q in (2 * c, 2 * c + 1):
-                    quantise_squares(q)
-            else:
-                quantise_squares(c + 8)
-                quantise_weight(c + 8)
-            if c == 9:
-                for a in range(TOKEN_TILES):
-                    scale_y(0, a)
-            if c == 10:
-                for a in range(TOKEN_TILES):
-                    add_bias_and_store(0, a)
-            if c <= 6:
-                for q in (2 * c + 2, 2 * c + 3):
-                    square_on_scalar(q, C1, C2)
-                    square_on_vector(q, C2, W_COLS)
-            if c >= 5:
-                square_apart(nsq, sq_pool, C3)
-                nsq += 1
-
-        for w in range(PASSES + 7, W_PASSES):
-            for a in range(TOKEN_TILES):
-                multiply_squares(w, a)
-            if w == W_PASSES - 1:
-                for a in range(TOKEN_TILES):
-                    demodulation(1, a)
-            for a in range(TOKEN_TILES):
-                multiply_weight(w, a)
-            if w + 1 < W_PASSES:
-                quantise_squares(w + 1)
-                quantise_weight(w + 1)
-            if nsq < W_PASSES:
-                square_apart(nsq, sq_pool, C4)
-                nsq += 1
+                    store(0, a)
+            c += 1
         for a in range(TOKEN_TILES):
             scale_y(1, a)
         for a in range(TOKEN_TILES):
-            add_bias_and_store(1, a)
+            add_bias(1, a)
+            store(1, a)

@@ -37,10 +37,11 @@ KEPT = 17
 UNITS = 3
 
 C0 = 640
-C1 = 1344
-C2 = 1728
-C3 = 896
+C1 = 1536
+C2 = 2048
+C3 = 1152
 
+GPSIMD_TOKENS = 256
 TURNED = (0, 1)
 X_BANKS = (2, 3)
 S_BANKS = (4, 5)
@@ -319,10 +320,16 @@ def tile_modulatedlinear_k_kernel(tc, x, modulation, weight, bias, mod_w, mod_b,
                 squares = prod_grouped[g][:, TOKENS * 4 :].rearrange(
                     "p (t u e) -> p t u e", u=2, e=2
                 )
-                if g < PASSES - 1:
-                    nc.gpsimd.tensor_tensor(out=squares, in0=s_view, in1=s_view, op=ALU.mult)
-                else:
-                    nc.scalar.activation(out=squares, in_=s_view, func=ACT.Square)
+                on_gpsimd = GPSIMD_TOKENS if g < PASSES - 1 else 0
+                if on_gpsimd > 0:
+                    part = s_view[:, :on_gpsimd]
+                    nc.gpsimd.tensor_tensor(
+                        out=squares[:, :on_gpsimd], in0=part, in1=part, op=ALU.mult
+                    )
+                if on_gpsimd < TOKENS:
+                    nc.scalar.activation(
+                        out=squares[:, on_gpsimd:], in_=s_view[:, on_gpsimd:], func=ACT.Square
+                    )
 
             def quantise_products(g):
                 kept = slice(g * 2 * TOKENS, (g + 1) * 2 * TOKENS)
@@ -434,7 +441,7 @@ def tile_modulatedlinear_k_kernel(tc, x, modulation, weight, bias, mod_w, mod_b,
             quantise_weight(PASSES - 1)
             square_on_scalar(PASSES - 1, 0, C1)
             quantise_squares(1)
-            for q in (2, 3):
+            for q in (2, 3, 4):
                 square_on_vector(q, C1, W_COLS)
             for a in range(TOKEN_TILES):
                 multiply_weight(PASSES - 2, a)
@@ -445,7 +452,8 @@ def tile_modulatedlinear_k_kernel(tc, x, modulation, weight, bias, mod_w, mod_b,
                 multiply_squares(1, a)
             for q in (2, 3, 4):
                 quantise_squares(q)
-                square_on_vector(q + 2, C1, W_COLS)
+            for q in (5, 6, 7):
+                square_on_vector(q, C1, W_COLS)
             for a in range(TOKEN_TILES):
                 multiply_weight(PASSES - 1, a)
 
@@ -472,13 +480,15 @@ def tile_modulatedlinear_k_kernel(tc, x, modulation, weight, bias, mod_w, mod_b,
             for kind, w in quantised[v : v + UNITS]:
                 if kind == "q":
                     quantise_squares(w)
-                    if w + 2 < PASSES:
-                        square_on_scalar(w + 2, C1, C2)
-                        square_on_vector(w + 2, C2, W_COLS)
                 else:
                     quantise_weight(w)
+            for kind, w in quantised[v : v + UNITS]:
+                if kind == "y":
                     square_on_scalar(w, 0, C3)
                     square_on_vector(w, C3, W_COLS)
+                elif w + UNITS < PASSES:
+                    square_on_scalar(w + UNITS, C1, C2)
+                    square_on_vector(w + UNITS, C2, W_COLS)
             v += UNITS
             for kind, w in multiplied[m : m + UNITS]:
                 for a in range(TOKEN_TILES):

@@ -32,16 +32,16 @@ W_COLS = ROUND_OUT * 4
 X_LOAD = 2
 W_LOAD = 2
 AHEAD = 2
-KEPT = 17
+KEPT = 13
 
 UNITS = 3
 
 C0 = 640
 C1 = 1536
-C2 = 2048
-C3 = 1152
+C2 = 1792
+C3 = 896
 
-GPSIMD_TOKENS = 256
+GPSIMD_TOKENS = 208
 TURNED = (0, 1)
 X_BANKS = (2, 3)
 S_BANKS = (4, 5)
@@ -133,6 +133,9 @@ def tile_modulatedlinear_k_kernel(tc, x, modulation, weight, bias, mod_w, mod_b,
                 )
             w_grouped[w] = grouped
 
+        def squared_early(w):
+            return w < 6 and w % 4 < 4
+
         def square_on_scalar(w, first, end):
             if end > first:
                 cols = w_grouped[w][:, first:end]
@@ -152,10 +155,10 @@ def tile_modulatedlinear_k_kernel(tc, x, modulation, weight, bias, mod_w, mod_b,
             return codes, scales
 
         def quantise_weight(w):
-            w_quantised[w] = quantise(w_grouped[w], "w", 6)
+            w_quantised[w] = quantise(w_grouped[w], "w", 7)
 
         def quantise_squares(w):
-            w2_quantised[w] = quantise(w_grouped[w], "w2", 6)
+            w2_quantised[w] = quantise(w_grouped[w], "w2", 11)
 
         def multiply_into(sums, product, moving, w, a):
             g = w % PASSES
@@ -396,6 +399,8 @@ def tile_modulatedlinear_k_kernel(tc, x, modulation, weight, bias, mod_w, mod_b,
                     quantise_products(i - 4)
                 if i >= 3:
                     quantise_weight(i - 3)
+                    if i >= 5 and squared_early(i - 5):
+                        quantise_squares(i - 5)
                     multiply_x(i - 3)
                     square_s(i - 3)
                     square_on_scalar(i - 3, 0, C0)
@@ -416,9 +421,10 @@ def tile_modulatedlinear_k_kernel(tc, x, modulation, weight, bias, mod_w, mod_b,
                 if i < PASSES:
                     quantise_mod_w(i)
                 if i >= 3:
-                    square_on_scalar(i - 3, C0, C1)
+                    square_on_scalar(i - 3, C0, W_COLS if squared_early(i - 3) else C1)
 
-            square_on_vector(0, C1, W_COLS)
+            early = [w for w in range(PASSES) if squared_early(w)]
+            later = [w for w in range(PASSES) if not squared_early(w)]
             turn_weight(PASSES)
             turn_x(PASSES - 1, 1)
             quantise_products(PASSES - 3)
@@ -429,38 +435,39 @@ def tile_modulatedlinear_k_kernel(tc, x, modulation, weight, bias, mod_w, mod_b,
             square_on_scalar(PASSES - 2, 0, C1)
             for a in range(TOKEN_TILES):
                 multiply_weight(PASSES - 3, a)
-            quantise_squares(0)
-            square_on_vector(1, C1, W_COLS)
+            for w in later[:2]:
+                square_on_vector(w, C1, W_COLS)
 
             turn_weight(PASSES + 1)
             quantise_products(PASSES - 2)
+            quantise_weight(PASSES - 1)
             multiply_x(PASSES - 1)
             square_s(PASSES - 1)
-            for a in range(TOKEN_TILES):
-                multiply_squares(0, a)
-            quantise_weight(PASSES - 1)
+            for w in early[:2]:
+                for a in range(TOKEN_TILES):
+                    multiply_squares(w, a)
             square_on_scalar(PASSES - 1, 0, C1)
-            quantise_squares(1)
-            for q in (2, 3, 4):
-                square_on_vector(q, C1, W_COLS)
+            for w in later[2:4]:
+                square_on_vector(w, C1, W_COLS)
             for a in range(TOKEN_TILES):
                 multiply_weight(PASSES - 2, a)
 
             turn_weight(PASSES + 2)
             quantise_products(PASSES - 1)
-            for a in range(TOKEN_TILES):
-                multiply_squares(1, a)
-            for q in (2, 3, 4):
-                quantise_squares(q)
-            for q in (5, 6, 7):
-                square_on_vector(q, C1, W_COLS)
+            for w in early[2:4]:
+                for a in range(TOKEN_TILES):
+                    multiply_squares(w, a)
+            for w in later[:2]:
+                quantise_squares(w)
+            for w in later[4:6]:
+                square_on_vector(w, C1, W_COLS)
             for a in range(TOKEN_TILES):
                 multiply_weight(PASSES - 1, a)
 
         late_y = list(range(PASSES, W_PASSES))
         late_q = list(range(PASSES, W_PASSES))
-        quantised = [("q", w) for w in range(5, PASSES)]
-        multiplied = [("q", w) for w in range(2, PASSES)]
+        quantised = [("q", w) for w in later[2:]]
+        multiplied = [("q", w) for w in early[4:] + later]
         for k in range(W_PASSES - PASSES + 2):
             if k < len(late_y):
                 quantised.append(("y", late_y[k]))
@@ -477,19 +484,29 @@ def tile_modulatedlinear_k_kernel(tc, x, modulation, weight, bias, mod_w, mod_b,
             if turned < W_PASSES:
                 turn_weight(turned)
                 turned += 1
-            for kind, w in quantised[v : v + UNITS]:
-                if kind == "q":
-                    quantise_squares(w)
-                else:
-                    quantise_weight(w)
-            for kind, w in quantised[v : v + UNITS]:
-                if kind == "y":
-                    square_on_scalar(w, 0, C3)
-                    square_on_vector(w, C3, W_COLS)
-                elif w + UNITS < PASSES:
-                    square_on_scalar(w + UNITS, C1, C2)
-                    square_on_vector(w + UNITS, C2, W_COLS)
-            v += UNITS
+            needed = multiplied[: m + UNITS + 4]
+            behind = True
+            while behind:
+                fresh = []
+                while v < len(quantised) and quantised[v] in needed:
+                    kind, w = quantised[v]
+                    if kind == "y" and w >= turned or ("y", w) in fresh:
+                        break
+                    fresh.append((kind, w))
+                    v += 1
+                for kind, w in fresh:
+                    if kind == "q":
+                        quantise_squares(w)
+                    else:
+                        quantise_weight(w)
+                for kind, w in fresh:
+                    if kind == "y":
+                        square_on_scalar(w, 0, C3)
+                        square_on_vector(w, C3, W_COLS)
+                    elif w + 4 < PASSES:
+                        square_on_scalar(w + 4, C1, C2)
+                        square_on_vector(w + 4, C2, W_COLS)
+                behind = any(unit in quantised[v:] for unit in multiplied[m : m + UNITS])
             for kind, w in multiplied[m : m + UNITS]:
                 for a in range(TOKEN_TILES):
                     (multiply_squares if kind == "q" else multiply_weight)(w, a)

@@ -31,24 +31,30 @@ W_COLS = ROUND_OUT * 4
 
 X_LOAD = 2
 W_LOAD = 2
-AHEAD = 2
+LOADS_AHEAD = 2
+BIAS_TURN = 6
+
+EARLY = 6
 KEPT = 13
+QUANTISED_WEIGHT = 7
+QUANTISED_SQUARES = 11
 
-UNITS = 3
+MULTIPLIED = 3
+LEAD = 4
+WEIGHT_LEAD = 2
 
-C0 = 640
-C1 = 1536
-C2 = 1792
-C3 = 896
+SCALAR_PIECE = 768
+SCALAR_FIRST = 1408
+SCALAR_ROUND_1 = 896
+SCALAR_LAST = 1280
 
 GPSIMD_TOKENS = 208
-TURNED = (0, 1)
+
+TURNED_BANKS = (0, 1)
 X_BANKS = (2, 3)
 S_BANKS = (4, 5)
-Y_BANKS = ((6, 7), (2, 3))
-Q_BANKS = ((4, 5), (4, 5))
-
-FLOPS = 2 * TOKENS * (MOD_DIM * IN_DIM + 2 * IN_DIM * OUT_DIM)
+Y_BANKS = ((6, 7), X_BANKS)
+Q_BANKS = (S_BANKS, S_BANKS)
 
 
 def transpose_words(nc, bank_cols, rows_bf16, first_word, u, ident):
@@ -116,11 +122,11 @@ def tile_modulatedlinear_k_kernel(tc, x, modulation, weight, bias, mod_w, mod_b,
                 load_weight(len(w_raw))
 
         def turn_weight(w):
-            load_weights_to(w + AHEAD)
+            load_weights_to(w + LOADS_AHEAD)
             grouped = w_kept.tile([P, W_COLS], BF16, align_bytes=64, name="w_grouped")
             words = grouped[:].bitcast(F32).rearrange("p (n o u) -> p n o u", n=2, u=2)
             for n in range(2):
-                w_bank = bank(TURNED[n])
+                w_bank = bank(TURNED_BANKS[n])
                 for u in range(2):
                     for b in range(2):
                         transpose_words(
@@ -133,18 +139,13 @@ def tile_modulatedlinear_k_kernel(tc, x, modulation, weight, bias, mod_w, mod_b,
                 )
             w_grouped[w] = grouped
 
-        def squared_early(w):
-            return w < 6 and w % 4 < 4
-
         def square_on_scalar(w, first, end):
-            if end > first:
-                cols = w_grouped[w][:, first:end]
-                nc.scalar.activation(out=cols, in_=cols, func=ACT.Square)
+            cols = w_grouped[w][:, first:end]
+            nc.scalar.activation(out=cols, in_=cols, func=ACT.Square)
 
         def square_on_vector(w, first, end):
-            if end > first:
-                cols = w_grouped[w][:, first:end]
-                nc.vector.tensor_tensor(out=cols, in0=cols, in1=cols, op=ALU.mult)
+            cols = w_grouped[w][:, first:end]
+            nc.vector.tensor_tensor(out=cols, in0=cols, in1=cols, op=ALU.mult)
 
         def quantise(values, kind, bufs):
             codes = w_work.tile([P, ROUND_OUT], U32, align_bytes=64, name=kind + "_codes", bufs=bufs)
@@ -155,16 +156,16 @@ def tile_modulatedlinear_k_kernel(tc, x, modulation, weight, bias, mod_w, mod_b,
             return codes, scales
 
         def quantise_weight(w):
-            w_quantised[w] = quantise(w_grouped[w], "w", 7)
+            w_quantised[w] = quantise(w_grouped[w], "w", QUANTISED_WEIGHT)
 
         def quantise_squares(w):
-            w2_quantised[w] = quantise(w_grouped[w], "w2", 11)
+            w2_quantised[w] = quantise(w_grouped[w], "w2", QUANTISED_SQUARES)
 
         def multiply_into(sums, product, moving, w, a):
             g = w % PASSES
             first = (2 * g + product) * TOKENS + a * P
             nc.tensor.matmul_mx(
-                out=sums[a][:],
+                out=sums[:],
                 lhsT=prod_codes[:, first : first + P].bitcast(FP8X4),
                 lhsT_scale=prod_scales[:, first : first + P],
                 rhs=moving[0][:].bitcast(FP8X4),
@@ -176,14 +177,14 @@ def tile_modulatedlinear_k_kernel(tc, x, modulation, weight, bias, mod_w, mod_b,
         def multiply_weight(w, a):
             if w % PASSES == 0:
                 y_sums[w // PASSES, a] = bank(Y_BANKS[w // PASSES][a])
-            multiply_into({a: y_sums[w // PASSES, a]}, 0, w_quantised[w], w, a)
+            multiply_into(y_sums[w // PASSES, a], 0, w_quantised[w], w, a)
 
         def multiply_squares(w, a):
             if w % PASSES == 0:
                 q_sums[w // PASSES, a] = bank(Q_BANKS[w // PASSES][a])
-            multiply_into({a: q_sums[w // PASSES, a]}, 1, w2_quantised[w], w, a)
+            multiply_into(q_sums[w // PASSES, a], 1, w2_quantised[w], w, a)
 
-        def demodulation(h, a):
+        def demodulate(h, a):
             demod = tail.tile([P, ROUND_OUT], F32, name="demod")
             nc.scalar.activation(
                 out=demod[:], in_=q_sums[h, a][:], func=ACT.Abs_reciprocal_sqrt, bias=eps[:]
@@ -250,7 +251,7 @@ def tile_modulatedlinear_k_kernel(tc, x, modulation, weight, bias, mod_w, mod_b,
                 grouped = work.tile([P, 4 * P * 4], BF16, align_bytes=64, name="mw_grouped", bufs=2)
                 words = grouped[:].bitcast(F32).rearrange("p (u e r v) -> p u e r v", u=2, e=2, v=2)
                 for u in range(2):
-                    mw_bank = bank(TURNED[u])
+                    mw_bank = bank(TURNED_BANKS[u])
                     for e in range(2):
                         for v in range(2):
                             transpose_words(
@@ -329,10 +330,9 @@ def tile_modulatedlinear_k_kernel(tc, x, modulation, weight, bias, mod_w, mod_b,
                     nc.gpsimd.tensor_tensor(
                         out=squares[:, :on_gpsimd], in0=part, in1=part, op=ALU.mult
                     )
-                if on_gpsimd < TOKENS:
-                    nc.scalar.activation(
-                        out=squares[:, on_gpsimd:], in_=s_view[:, on_gpsimd:], func=ACT.Square
-                    )
+                nc.scalar.activation(
+                    out=squares[:, on_gpsimd:], in_=s_view[:, on_gpsimd:], func=ACT.Square
+                )
 
             def quantise_products(g):
                 kept = slice(g * 2 * TOKENS, (g + 1) * 2 * TOKENS)
@@ -350,11 +350,11 @@ def tile_modulatedlinear_k_kernel(tc, x, modulation, weight, bias, mod_w, mod_b,
                 out=mod_b_raw[:PASSES, :], in_=mod_b.rearrange("(g k) -> g k", k=K_PASS)
             )
             load_mod_w_to(1)
-            load_x_to(0)
             load_weights_to(0)
+            load_x_to(0)
             load_mod_w_to(2)
 
-            mod_bank = bank(6)
+            mod_bank = bank(Y_BANKS[0][0])
             for u in range(2):
                 for a in range(TOKEN_TILES):
                     transpose_words(
@@ -373,7 +373,7 @@ def tile_modulatedlinear_k_kernel(tc, x, modulation, weight, bias, mod_w, mod_b,
             )
 
             def turn_mod_b():
-                mod_b_bank = bank(7)
+                mod_b_bank = bank(Y_BANKS[0][1])
                 for u in range(2):
                     transpose_words(
                         nc, mod_b_bank[:, u * P : (u + 1) * P], mod_b_raw[:], 0, u, ident[:]
@@ -387,9 +387,9 @@ def tile_modulatedlinear_k_kernel(tc, x, modulation, weight, bias, mod_w, mod_b,
                     )
 
             for i in range(PASSES + 1):
-                load_mod_w_to(i + AHEAD)
-                load_x_to(i - 1 + AHEAD)
-                if i == 6:
+                load_mod_w_to(i + LOADS_AHEAD)
+                load_x_to(i - 1 + LOADS_AHEAD)
+                if i == BIAS_TURN:
                     nc.sync.dma_start(out=bias_all[:], in_=bias.partition_broadcast(P))
                 if i < PASSES:
                     turn_mod_w(i)
@@ -399,11 +399,11 @@ def tile_modulatedlinear_k_kernel(tc, x, modulation, weight, bias, mod_w, mod_b,
                     quantise_products(i - 4)
                 if i >= 3:
                     quantise_weight(i - 3)
-                    if i >= 5 and squared_early(i - 5):
+                    if 5 <= i < 5 + EARLY:
                         quantise_squares(i - 5)
                     multiply_x(i - 3)
                     square_s(i - 3)
-                    square_on_scalar(i - 3, 0, C0)
+                    square_on_scalar(i - 3, 0, SCALAR_PIECE)
                 if i >= 2:
                     add_mod_b(i - 2, 1)
                     turn_x(i - 2, 1)
@@ -421,10 +421,8 @@ def tile_modulatedlinear_k_kernel(tc, x, modulation, weight, bias, mod_w, mod_b,
                 if i < PASSES:
                     quantise_mod_w(i)
                 if i >= 3:
-                    square_on_scalar(i - 3, C0, W_COLS if squared_early(i - 3) else C1)
+                    square_on_scalar(i - 3, SCALAR_PIECE, W_COLS if i - 3 < EARLY else SCALAR_FIRST)
 
-            early = [w for w in range(PASSES) if squared_early(w)]
-            later = [w for w in range(PASSES) if not squared_early(w)]
             turn_weight(PASSES)
             turn_x(PASSES - 1, 1)
             quantise_products(PASSES - 3)
@@ -432,97 +430,96 @@ def tile_modulatedlinear_k_kernel(tc, x, modulation, weight, bias, mod_w, mod_b,
             multiply_x(PASSES - 2)
             square_s(PASSES - 2)
             add_mod_b(PASSES - 1, 1)
-            square_on_scalar(PASSES - 2, 0, C1)
+            square_on_scalar(PASSES - 2, 0, SCALAR_FIRST)
             for a in range(TOKEN_TILES):
                 multiply_weight(PASSES - 3, a)
-            for w in later[:2]:
-                square_on_vector(w, C1, W_COLS)
+            for w in (EARLY, EARLY + 1):
+                square_on_vector(w, SCALAR_FIRST, W_COLS)
 
             turn_weight(PASSES + 1)
             quantise_products(PASSES - 2)
             quantise_weight(PASSES - 1)
             multiply_x(PASSES - 1)
             square_s(PASSES - 1)
-            for w in early[:2]:
+            for w in (0, 1):
                 for a in range(TOKEN_TILES):
                     multiply_squares(w, a)
-            square_on_scalar(PASSES - 1, 0, C1)
-            for w in later[2:4]:
-                square_on_vector(w, C1, W_COLS)
+            square_on_scalar(PASSES - 1, 0, SCALAR_FIRST)
+            for w in (EARLY + 2, EARLY + 3):
+                square_on_vector(w, SCALAR_FIRST, W_COLS)
             for a in range(TOKEN_TILES):
                 multiply_weight(PASSES - 2, a)
 
             turn_weight(PASSES + 2)
             quantise_products(PASSES - 1)
-            for w in early[2:4]:
+            for w in (2, 3):
                 for a in range(TOKEN_TILES):
                     multiply_squares(w, a)
-            for w in later[:2]:
+            for w in (EARLY, EARLY + 1):
                 quantise_squares(w)
-            for w in later[4:6]:
-                square_on_vector(w, C1, W_COLS)
+            for w in (EARLY + 4, EARLY + 5):
+                square_on_vector(w, SCALAR_FIRST, W_COLS)
             for a in range(TOKEN_TILES):
                 multiply_weight(PASSES - 1, a)
 
-        late_y = list(range(PASSES, W_PASSES))
-        late_q = list(range(PASSES, W_PASSES))
-        quantised = [("q", w) for w in later[2:]]
-        multiplied = [("q", w) for w in early[4:] + later]
-        for k in range(W_PASSES - PASSES + 2):
-            if k < len(late_y):
-                quantised.append(("y", late_y[k]))
-            if k >= 2:
-                quantised.append(("q", late_q[k - 2]))
-        multiplied += [u for u in quantised if u[1] >= PASSES and not (u[0] == "y" and u[1] >= W_PASSES - 2)]
-        multiplied += [("y", W_PASSES - 2), ("y", W_PASSES - 1)]
+        round_1 = []
+        for w in range(PASSES, W_PASSES + WEIGHT_LEAD):
+            if w < W_PASSES:
+                round_1.append(("y", w))
+            if w - WEIGHT_LEAD >= PASSES:
+                round_1.append(("q", w - WEIGHT_LEAD))
+        last = [("y", W_PASSES - 2), ("y", W_PASSES - 1)]
+        to_quantise = [("q", w) for w in range(EARLY + 2, PASSES)] + round_1
+        to_multiply = [("q", w) for w in range(4, PASSES)]
+        to_multiply += [step for step in round_1 if step not in last] + last
+
         turned = PASSES + 3
-        m = 0
-        v = 0
-        finish_at = {}
-        c = 0
-        while m < len(multiplied):
+        quantised = 0
+        finish_in = {}
+        for turn in range(-(-len(to_multiply) // MULTIPLIED)):
+            now = to_multiply[turn * MULTIPLIED : (turn + 1) * MULTIPLIED]
+            soon = to_multiply[: (turn + 1) * MULTIPLIED + LEAD]
             if turned < W_PASSES:
                 turn_weight(turned)
                 turned += 1
-            needed = multiplied[: m + UNITS + 4]
             behind = True
             while behind:
-                fresh = []
-                while v < len(quantised) and quantised[v] in needed:
-                    kind, w = quantised[v]
-                    if kind == "y" and w >= turned or ("y", w) in fresh:
+                run = []
+                while quantised < len(to_quantise) and to_quantise[quantised] in soon:
+                    kind, w = to_quantise[quantised]
+                    if kind == "y" and w >= turned or ("y", w) in run:
                         break
-                    fresh.append((kind, w))
-                    v += 1
-                for kind, w in fresh:
+                    run.append((kind, w))
+                    quantised += 1
+                for kind, w in run:
                     if kind == "q":
                         quantise_squares(w)
                     else:
                         quantise_weight(w)
-                for kind, w in fresh:
+                for kind, w in run:
                     if kind == "y":
-                        square_on_scalar(w, 0, C3)
-                        square_on_vector(w, C3, W_COLS)
+                        split = SCALAR_LAST if (kind, w) in last else SCALAR_ROUND_1
+                        square_on_scalar(w, 0, split)
+                        square_on_vector(w, split, W_COLS)
                     elif w + 4 < PASSES:
-                        square_on_scalar(w + 4, C1, C2)
-                        square_on_vector(w + 4, C2, W_COLS)
-                behind = any(unit in quantised[v:] for unit in multiplied[m : m + UNITS])
-            for kind, w in multiplied[m : m + UNITS]:
+                        square_on_scalar(w + 4, SCALAR_FIRST, W_COLS)
+                behind = any(step in to_quantise[quantised:] for step in now)
+            for kind, w in now:
                 for a in range(TOKEN_TILES):
-                    (multiply_squares if kind == "q" else multiply_weight)(w, a)
+                    if kind == "q":
+                        multiply_squares(w, a)
+                    else:
+                        multiply_weight(w, a)
                 if kind == "q" and w % PASSES == PASSES - 1:
                     for a in range(TOKEN_TILES):
-                        demodulation(w // PASSES, a)
-                    if w < PASSES:
-                        finish_at = {c + 1: scale_y, c + 2: add_bias}
-            m += UNITS
-            if c in finish_at:
+                        demodulate(w // PASSES, a)
+                    finish_in = {turn + 1: scale_y, turn + 2: add_bias} if w < PASSES else {}
+            if turn in finish_in:
                 for a in range(TOKEN_TILES):
-                    finish_at[c](0, a)
-            if turned == W_PASSES - 2:
+                    finish_in[turn](0, a)
+            if turned + LOADS_AHEAD == W_PASSES:
                 for a in range(TOKEN_TILES):
                     store(0, a)
-            c += 1
         for a in range(TOKEN_TILES):
             scale_y(1, a)
         for a in range(TOKEN_TILES):

from contextlib import ExitStack

import concourse.mybir as mybir
from concourse.masks import make_identity

F32 = mybir.dt.float32
BF16 = mybir.dt.bfloat16
U32 = mybir.dt.uint32
U8 = mybir.dt.uint8
FP8X4 = mybir.dt.float8_e4m3fn_x4
ACT = mybir.ActivationFunctionType
ALU = mybir.AluOpType

P = 128
TOKENS = 256
IN_DIM = 8192
OUT_DIM = 1024
MOD_DIM = 512
EPS = 1e-8

K_PASS = 512
PASSES = IN_DIM // K_PASS
WORDS = K_PASS // 2
BANK = 512
TOKEN_TILES = TOKENS // P
ROUND_OUT = 512
ROUNDS = OUT_DIM // ROUND_OUT
ROW_TILES = ROUND_OUT // P
W_PASSES = ROUNDS * PASSES
W_COLS = ROUND_OUT * 4

X_LOAD = 2
W_LOAD = 2
LOADS_AHEAD = 2
BIAS_TURN = 6

EARLY = 6
KEPT = 13
QUANTISED_WEIGHT = 7
QUANTISED_SQUARES = 11

MULTIPLIED = 3
LEAD = 4
WEIGHT_LEAD = 2

SCALAR_PIECE = 768
SCALAR_FIRST = 1408
SCALAR_ROUND_1 = 896
SCALAR_LAST = 1280

GPSIMD_TOKENS = 208

TURNED_BANKS = (0, 1)
X_BANKS = (2, 3)
S_BANKS = (4, 5)
Y_BANKS = ((6, 7), X_BANKS)
Q_BANKS = (S_BANKS, S_BANKS)


def transpose_words(nc, bank_cols, rows_bf16, first_word, u, ident):
    nc.tensor.transpose(
        bank_cols, rows_bf16.bitcast(F32)[:, first_word + u : first_word + WORDS : 2], ident
    )


def tile_modulatedlinear_k_kernel(tc, x, modulation, weight, bias, mod_w, mod_b, out):
    nc = tc.nc
    x_rows = x.flatten_outer_dims().rearrange("(a r) i -> r a i", r=P)
    modulation_rows = modulation.flatten_outer_dims().rearrange("(a r) k -> r a k", r=P)
    out_rows = out.flatten_outer_dims()
    mod_w_rows = mod_w.rearrange("(g r j) k -> r g j k", r=P, j=4)
    weight_rows = weight.rearrange("(h b r) i -> r h b i", b=ROW_TILES, r=P)

    with ExitStack() as whole:
        whole.enter_context(tc.manual_schedule())
        const = whole.enter_context(tc.tile_pool(name="const", bufs=1))
        w_in = whole.enter_context(tc.tile_pool(name="w_in", bufs=3))
        w_kept = whole.enter_context(tc.tile_pool(name="w_kept", bufs=KEPT))
        w_work = whole.enter_context(tc.tile_pool(name="w_work", bufs=3))
        tail = whole.enter_context(tc.tile_pool(name="tail", bufs=2))
        psum = whole.enter_context(tc.psum_pool(name="psum", bufs=1))

        def bank(n):
            return psum.tile([P, BANK], F32, name="bank%d" % n)

        ident = const.tile([P, P], F32)
        make_identity(nc, ident[:])
        eps = const.tile([P, 1], F32)
        nc.vector.memset(eps[:], EPS)
        table_warm = const.tile([P, 1], F32)
        nc.scalar.activation(out=table_warm[:], in_=eps[:], func=ACT.Abs_reciprocal_sqrt)

        bias_all = const.tile([P, OUT_DIM], BF16)

        prod_codes = const.tile([P, PASSES * 2 * TOKENS], U32, align_bytes=64)
        prod_scales = const.tile([P, PASSES * 2 * TOKENS], U8, align_bytes=64)
        mod_b_cols = const.tile([P, 4 * PASSES], F32)

        w_raw = {}
        w_grouped = {}
        w_quantised = {}
        w2_quantised = {}
        y_sums = {}
        q_sums = {}
        demods = {}
        results = {}

        def load_weight(load):
            first = load * W_LOAD
            raw = w_in.tile([P, ROW_TILES, W_LOAD * K_PASS], BF16, name="w_raw")
            nc.sync.dma_start(
                out=raw[:],
                in_=weight_rows[
                    :, first // PASSES, :,
                    (first % PASSES) * K_PASS : (first % PASSES + W_LOAD) * K_PASS,
                ],
            )
            w_raw[load] = raw

        def load_weights_to(w):
            while len(w_raw) * W_LOAD <= min(w, W_PASSES - 1):
                load_weight(len(w_raw))

        def turn_weight(w):
            load_weights_to(w + LOADS_AHEAD)
            grouped = w_kept.tile([P, W_COLS], BF16, align_bytes=64, name="w_grouped")
            words = grouped[:].bitcast(F32).rearrange("p (n o u) -> p n o u", n=2, u=2)
            for n in range(2):
                w_bank = bank(TURNED_BANKS[n])
                for u in range(2):
                    for b in range(2):
                        transpose_words(
                            nc, w_bank[:, (2 * u + b) * P : (2 * u + b + 1) * P],
                            w_raw[w // W_LOAD][:, 2 * n + b, :],
                            (w % W_LOAD) * WORDS, u, ident[:],
                        )
                nc.scalar.copy(
                    out=words[:, n], in_=w_bank[:].rearrange("p (u o) -> p o u", u=2)
                )
            w_grouped[w] = grouped

        def square_on_scalar(w, first, end):
            cols = w_grouped[w][:, first:end]
            nc.scalar.activation(out=cols, in_=cols, func=ACT.Square)

        def square_on_vector(w, first, end):
            cols = w_grouped[w][:, first:end]
            nc.vector.tensor_tensor(out=cols, in0=cols, in1=cols, op=ALU.mult)

        def quantise(values, kind, bufs):
            codes = w_work.tile([P, ROUND_OUT], U32, align_bytes=64, name=kind + "_codes", bufs=bufs)
            scales = w_work.tile([P, ROUND_OUT], U8, align_bytes=64, name=kind + "_scales", bufs=bufs)
            nc.vector.quantize_mx(
                out=codes[:].bitcast(FP8X4), scales=scales[:], in_=values[:]
            )
            return codes, scales

        def quantise_weight(w):
            w_quantised[w] = quantise(w_grouped[w], "w", QUANTISED_WEIGHT)

        def quantise_squares(w):
            w2_quantised[w] = quantise(w_grouped[w], "w2", QUANTISED_SQUARES)

        def multiply_into(sums, product, moving, w, a):
            g = w % PASSES
            first = (2 * g + product) * TOKENS + a * P
            nc.tensor.matmul_mx(
                out=sums[:],
                lhsT=prod_codes[:, first : first + P].bitcast(FP8X4),
                lhsT_scale=prod_scales[:, first : first + P],
                rhs=moving[0][:].bitcast(FP8X4),
                rhs_scale=moving[1][:],
                start=(g == 0),
                stop=(g == PASSES - 1),
            )

        def multiply_weight(w, a):
            if w % PASSES == 0:
                y_sums[w // PASSES, a] = bank(Y_BANKS[w // PASSES][a])
            multiply_into(y_sums[w // PASSES, a], 0, w_quantised[w], w, a)

        def multiply_squares(w, a):
            if w % PASSES == 0:
                q_sums[w // PASSES, a] = bank(Q_BANKS[w // PASSES][a])
            multiply_into(q_sums[w // PASSES, a], 1, w2_quantised[w], w, a)

        def demodulate(h, a):
            demod = tail.tile([P, ROUND_OUT], F32, name="demod")
            nc.scalar.activation(
                out=demod[:], in_=q_sums[h, a][:], func=ACT.Abs_reciprocal_sqrt, bias=eps[:]
            )
            demods[h, a] = demod

        def scale_y(h, a):
            result = tail.tile([P, ROUND_OUT], F32, name="result")
            nc.vector.tensor_tensor(
                out=result[:], in0=y_sums[h, a][:], in1=demods[h, a][:], op=ALU.mult
            )
            results[h, a] = result

        def add_bias(h, a):
            nc.vector.tensor_tensor(
                out=results[h, a][:], in0=results[h, a][:],
                in1=bias_all[:, h * ROUND_OUT : (h + 1) * ROUND_OUT], op=ALU.add,
            )

        def store(h, a):
            nc.sync.dma_start(
                out=out_rows[a * P : (a + 1) * P, h * ROUND_OUT : (h + 1) * ROUND_OUT],
                in_=results[h, a][:],
            )

        with ExitStack() as stage1:
            once = stage1.enter_context(tc.tile_pool(name="once", bufs=1))
            mw_in = stage1.enter_context(tc.tile_pool(name="mw_in", bufs=3))
            x_in = stage1.enter_context(tc.tile_pool(name="x_in", bufs=3))
            work = stage1.enter_context(tc.tile_pool(name="work", bufs=3))

            x_raw = {}
            mw_raw = {}
            mw_grouped = {}
            mw_codes = {}
            mw_scales = {}
            x_banks = {}
            s_banks = {}
            s_values = {}
            prod_grouped = {}

            def load_mod_w(g):
                raw = mw_in.tile([P, 4, MOD_DIM], BF16, name="mw_raw")
                nc.sync.dma_start(out=raw[:], in_=mod_w_rows[:, g, :, :])
                mw_raw[g] = raw

            def load_x(load):
                raw = x_in.tile([P, TOKEN_TILES, X_LOAD * K_PASS], BF16, name="x_raw")
                nc.sync.dma_start(
                    out=raw[:],
                    in_=x_rows[:, :, load * X_LOAD * K_PASS : (load + 1) * X_LOAD * K_PASS],
                )
                x_raw[load] = raw

            def load_mod_w_to(g):
                while len(mw_raw) <= min(g, PASSES - 1):
                    load_mod_w(len(mw_raw))

            def load_x_to(g):
                while len(x_raw) * X_LOAD <= min(g, PASSES - 1):
                    load_x(len(x_raw))

            def turn_mod_w(g):
                grouped = work.tile([P, 4 * P * 4], BF16, align_bytes=64, name="mw_grouped", bufs=2)
                words = grouped[:].bitcast(F32).rearrange("p (u e r v) -> p u e r v", u=2, e=2, v=2)
                for u in range(2):
                    mw_bank = bank(TURNED_BANKS[u])
                    for e in range(2):
                        for v in range(2):
                            transpose_words(
                                nc, mw_bank[:, (2 * e + v) * P : (2 * e + v + 1) * P],
                                mw_raw[g][:, 2 * u + e, :], 0, v, ident[:],
                            )
                    nc.scalar.copy(
                        out=words[:, u], in_=mw_bank[:].rearrange("p (e v r) -> p e r v", e=2, v=2)
                    )
                mw_grouped[g] = grouped

            def quantise_mod_w(g):
                codes = work.tile([P, 4 * P], U32, align_bytes=64, name="mw_codes", bufs=2)
                scales = work.tile([P, 4 * P], U8, align_bytes=64, name="mw_scales", bufs=2)
                nc.vector.quantize_mx(
                    out=codes[:].bitcast(FP8X4), scales=scales[:], in_=mw_grouped[g][:]
                )
                mw_codes[g] = codes
                mw_scales[g] = scales

            def turn_x(g, u):
                if u == 0:
                    x_banks[g] = bank(X_BANKS[g % 2])
                for a in range(TOKEN_TILES):
                    transpose_words(
                        nc, x_banks[g][:, (u * TOKEN_TILES + a) * P : (u * TOKEN_TILES + a + 1) * P],
                        x_raw[g // X_LOAD][:, a, :], (g % X_LOAD) * WORDS, u, ident[:],
                    )

            def first_matmul(g, u):
                s_bank = bank(S_BANKS[u])
                for e in range(2):
                    j = 2 * u + e
                    nc.tensor.matmul_mx(
                        out=s_bank[:, e * TOKENS : (e + 1) * TOKENS],
                        lhsT=mw_codes[g][:, j * P : (j + 1) * P].bitcast(FP8X4),
                        lhsT_scale=mw_scales[g][:, j * P : (j + 1) * P],
                        rhs=mod_codes[:].bitcast(FP8X4),
                        rhs_scale=mod_scales[:],
                        start=True,
                        stop=True,
                    )
                s_banks[g, u] = s_bank

            def add_mod_b(g, u):
                if u == 0:
                    s_sb = work.tile([P, 4 * TOKENS], F32, name="s_sb", bufs=4)
                    s_values[g] = s_sb
                nc.vector.tensor_tensor(
                    out=s_values[g][:, u * BANK : (u + 1) * BANK].rearrange("p (t e) -> p t e", e=2),
                    in0=s_banks[g, u][:].rearrange("p (e t) -> p t e", e=2),
                    in1=mod_b_cols[:, 4 * g + 2 * u : 4 * g + 2 * u + 2]
                    .unsqueeze(1)
                    .to_broadcast([P, TOKENS, 2]),
                    op=ALU.add,
                )

            def multiply_x(g):
                prod = work.tile([P, 2 * TOKENS * 4], BF16, align_bytes=64, name="prod_grouped", bufs=1)
                prod_grouped[g] = prod
                nc.vector.tensor_tensor(
                    out=prod[:, : TOKENS * 4].rearrange("p (t u e) -> p t u e", u=2, e=2),
                    in0=x_banks[g][:].bitcast(BF16).rearrange("p (u t e) -> p t u e", u=2, e=2),
                    in1=s_values[g][:].rearrange("p (u t e) -> p t u e", u=2, e=2),
                    op=ALU.mult,
                )

            def square_s(g):
                s_view = s_values[g][:].rearrange("p (u t e) -> p t u e", u=2, e=2)
                squares = prod_grouped[g][:, TOKENS * 4 :].rearrange(
                    "p (t u e) -> p t u e", u=2, e=2
                )
                on_gpsimd = GPSIMD_TOKENS if g < PASSES - 1 else 0
                if on_gpsimd > 0:
                    part = s_view[:, :on_gpsimd]
                    nc.gpsimd.tensor_tensor(
                        out=squares[:, :on_gpsimd], in0=part, in1=part, op=ALU.mult
                    )
                nc.scalar.activation(
                    out=squares[:, on_gpsimd:], in_=s_view[:, on_gpsimd:], func=ACT.Square
                )

            def quantise_products(g):
                kept = slice(g * 2 * TOKENS, (g + 1) * 2 * TOKENS)
                nc.vector.quantize_mx(
                    out=prod_codes[:, kept].bitcast(FP8X4), scales=prod_scales[:, kept],
                    in_=prod_grouped[g][:],
                )

            mod_raw = once.tile([P, TOKEN_TILES, MOD_DIM], BF16)
            nc.sync.dma_start(out=mod_raw[:], in_=modulation_rows)
            mod_b_raw = once.tile([P, K_PASS], BF16)
            nc.vector.memset(mod_b_raw[:], 0.0)
            load_mod_w_to(0)
            nc.sync.dma_start(
                out=mod_b_raw[:PASSES, :], in_=mod_b.rearrange("(g k) -> g k", k=K_PASS)
            )
            load_mod_w_to(1)
            load_weights_to(0)
            load_x_to(0)
            load_mod_w_to(2)

            mod_bank = bank(Y_BANKS[0][0])
            for u in range(2):
                for a in range(TOKEN_TILES):
                    transpose_words(
                        nc, mod_bank[:, (u * TOKEN_TILES + a) * P : (u * TOKEN_TILES + a + 1) * P],
                        mod_raw[:, a, :], 0, u, ident[:],
                    )
            mod_grouped = once.tile([P, TOKENS * 4], BF16, align_bytes=64)
            nc.vector.tensor_copy(
                out=mod_grouped[:].bitcast(F32).rearrange("p (t u) -> p t u", u=2),
                in_=mod_bank[:].rearrange("p (u t) -> p t u", u=2),
            )
            mod_codes = once.tile([P, TOKENS], U32, align_bytes=64)
            mod_scales = once.tile([P, TOKENS], U8, align_bytes=64)
            nc.vector.quantize_mx(
                out=mod_codes[:].bitcast(FP8X4), scales=mod_scales[:], in_=mod_grouped[:]
            )

            def turn_mod_b():
                mod_b_bank = bank(Y_BANKS[0][1])
                for u in range(2):
                    transpose_words(
                        nc, mod_b_bank[:, u * P : (u + 1) * P], mod_b_raw[:], 0, u, ident[:]
                    )
                for u in range(2):
                    nc.vector.tensor_copy(
                        out=mod_b_cols[:].rearrange("p (g u e) -> p g u e", u=2, e=2)[:, :, u, :],
                        in_=mod_b_bank[:, u * P : u * P + PASSES].bitcast(BF16).rearrange(
                            "p (g e) -> p g e", e=2
                        ),
                    )

            for i in range(PASSES + 1):
                load_mod_w_to(i + LOADS_AHEAD)
                load_x_to(i - 1 + LOADS_AHEAD)
                if i == BIAS_TURN:
                    nc.sync.dma_start(out=bias_all[:], in_=bias.partition_broadcast(P))
                if i < PASSES:
                    turn_mod_w(i)
                if i == 0:
                    turn_mod_b()
                if i >= 4:
                    quantise_products(i - 4)
                if i >= 3:
                    quantise_weight(i - 3)
                    if 5 <= i < 5 + EARLY:
                        quantise_squares(i - 5)
                    multiply_x(i - 3)
                    square_s(i - 3)
                    square_on_scalar(i - 3, 0, SCALAR_PIECE)
                if i >= 2:
                    add_mod_b(i - 2, 1)
                    turn_x(i - 2, 1)
                if i >= 1:
                    first_matmul(i - 1, 0)
                if i >= 4:
                    multiply_weight(i - 4, 0)
                if i >= 1:
                    turn_weight(i - 1)
                    turn_x(i - 1, 0)
                    add_mod_b(i - 1, 0)
                    first_matmul(i - 1, 1)
                if i >= 4:
                    multiply_weight(i - 4, 1)
                if i < PASSES:
                    quantise_mod_w(i)
                if i >= 3:
                    square_on_scalar(i - 3, SCALAR_PIECE, W_COLS if i - 3 < EARLY else SCALAR_FIRST)

            turn_weight(PASSES)
            turn_x(PASSES - 1, 1)
            quantise_products(PASSES - 3)
            quantise_weight(PASSES - 2)
            multiply_x(PASSES - 2)
            square_s(PASSES - 2)
            add_mod_b(PASSES - 1, 1)
            square_on_scalar(PASSES - 2, 0, SCALAR_FIRST)
            for a in range(TOKEN_TILES):
                multiply_weight(PASSES - 3, a)
            for w in (EARLY, EARLY + 1):
                square_on_vector(w, SCALAR_FIRST, W_COLS)

            turn_weight(PASSES + 1)
            quantise_products(PASSES - 2)
            quantise_weight(PASSES - 1)
            multiply_x(PASSES - 1)
            square_s(PASSES - 1)
            for w in (0, 1):
                for a in range(TOKEN_TILES):
                    multiply_squares(w, a)
            square_on_scalar(PASSES - 1, 0, SCALAR_FIRST)
            for w in (EARLY + 2, EARLY + 3):
                square_on_vector(w, SCALAR_FIRST, W_COLS)
            for a in range(TOKEN_TILES):
                multiply_weight(PASSES - 2, a)

            turn_weight(PASSES + 2)
            quantise_products(PASSES - 1)
            for w in (2, 3):
                for a in range(TOKEN_TILES):
                    multiply_squares(w, a)
            for w in (EARLY, EARLY + 1):
                quantise_squares(w)
            for w in (EARLY + 4, EARLY + 5):
                square_on_vector(w, SCALAR_FIRST, W_COLS)
            for a in range(TOKEN_TILES):
                multiply_weight(PASSES - 1, a)

        round_1 = []
        for w in range(PASSES, W_PASSES + WEIGHT_LEAD):
            if w < W_PASSES:
                round_1.append(("y", w))
            if w - WEIGHT_LEAD >= PASSES:
                round_1.append(("q", w - WEIGHT_LEAD))
        last = [("y", W_PASSES - 2), ("y", W_PASSES - 1)]
        to_quantise = [("q", w) for w in range(EARLY + 2, PASSES)] + round_1
        to_multiply = [("q", w) for w in range(4, PASSES)]
        to_multiply += [step for step in round_1 if step not in last] + last

        turned = PASSES + 3
        quantised = 0
        finish_in = {}
        for turn in range(-(-len(to_multiply) // MULTIPLIED)):
            now = to_multiply[turn * MULTIPLIED : (turn + 1) * MULTIPLIED]
            soon = to_multiply[: (turn + 1) * MULTIPLIED + LEAD]
            if turned < W_PASSES:
                turn_weight(turned)
                turned += 1
            behind = True
            while behind:
                run = []
                while quantised < len(to_quantise) and to_quantise[quantised] in soon:
                    kind, w = to_quantise[quantised]
                    if kind == "y" and w >= turned or ("y", w) in run:
                        break
                    run.append((kind, w))
                    quantised += 1
                for kind, w in run:
                    if kind == "q":
                        quantise_squares(w)
                    else:
                        quantise_weight(w)
                for kind, w in run:
                    if kind == "y":
                        split = SCALAR_LAST if (kind, w) in last else SCALAR_ROUND_1
                        square_on_scalar(w, 0, split)
                        square_on_vector(w, split, W_COLS)
                    elif w + 4 < PASSES:
                        square_on_scalar(w + 4, SCALAR_FIRST, W_COLS)
                behind = any(step in to_quantise[quantised:] for step in now)
            for kind, w in now:
                for a in range(TOKEN_TILES):
                    if kind == "q":
                        multiply_squares(w, a)
                    else:
                        multiply_weight(w, a)
                if kind == "q" and w % PASSES == PASSES - 1:
                    for a in range(TOKEN_TILES):
                        demodulate(w // PASSES, a)
                    finish_in = {turn + 1: scale_y, turn + 2: add_bias} if w < PASSES else {}
            if turn in finish_in:
                for a in range(TOKEN_TILES):
                    finish_in[turn](0, a)
            if turned + LOADS_AHEAD == W_PASSES:
                for a in range(TOKEN_TILES):
                    store(0, a)
        for a in range(TOKEN_TILES):
            scale_y(1, a)
        for a in range(TOKEN_TILES):
            add_bias(1, a)
            store(1, a)
